import numpy as np
import ml_dtypes


def mxq(x, axis, fmt="e4m3"):
    dtype, down = {"e4m3": (ml_dtypes.float8_e4m3fn, 7), "e5m2": (ml_dtypes.float8_e5m2, 14)}[fmt]
    v = np.moveaxis(np.asarray(x, np.float32).astype(ml_dtypes.bfloat16).astype(np.float64), axis, -1)
    blocks = v.reshape(v.shape[:-1] + (-1, 32))
    amax = np.abs(blocks).max(-1, keepdims=True)
    byte = np.maximum(np.where(amax > 0, np.frexp(amax)[1] - 1 + 127, 0) - down, 1)
    scale = np.exp2(byte - 127.0)
    codes = (blocks / scale).astype(np.float32).astype(dtype).astype(np.float64)
    return np.moveaxis((codes * scale).reshape(v.shape), -1, axis)


WIDE = False


def mx_kscale(k):
    if not WIDE:
        return np.ones(k)
    levels = np.array([10, -10, 5, -5, 0])
    a = np.random.permutation(np.resize(levels, k // 512 * 4)).reshape(k // 512, 4)
    idx = np.arange(k)
    return np.exp2(a[idx // 512, idx % 128 // 32])


BF16 = ml_dtypes.bfloat16


def bf(x):
    return np.asarray(x, np.float32).astype(BF16)


def f64(x):
    return np.asarray(x).astype(np.float64)


N, U0, U1, U2, F0, F1, F2, D1, D2 = 4096, 512, 128, 128, 1024, 512, 256, 3, 5


def silu(v):
    return v / (1.0 + np.exp(-v))


def norm_act(y, axis):
    n = np.sqrt(np.sum(y * y, axis=axis, keepdims=True))
    n_safe = np.where(n == 0, 1.0, n)
    return y * (silu(n) / n_safe)


def setup_inputs():
    s = mx_kscale(U0)
    x = np.random.standard_normal((N, U0 + U1 * D1))
    x[:, :U0] = x[:, :U0] * s
    return {"x": bf(x),
            "w1_l0": bf(np.random.standard_normal((U0, F0)) / s[:, None]),
            "w1_l1": bf(np.random.standard_normal((U1, F1))),
            "w2_l0": bf(np.random.standard_normal((F0, U0))),
            "w2_l1": bf(np.random.standard_normal((F1, U1)))}


def reference(x, w1_l0, w1_l1, w2_l0, w2_l1):
    x0 = f64(x)[:, :U0]
    y0 = (mxq(x0, 1, "e4m3") @ mxq(f64(w1_l0), 0, "e4m3")) * (1.0 / np.sqrt(U0))
    h0 = norm_act(y0[:, None, :], 1)[:, 0, :]
    o0 = (mxq(h0, 1, "e4m3") @ mxq(f64(w2_l0), 0, "e4m3")) * (1.0 / np.sqrt(F0))
    x1 = f64(x)[:, U0:].reshape(N, U1, D1).transpose(0, 2, 1)
    y1 = (x1 @ f64(w1_l1)) * (1.0 / np.sqrt(U1))
    h1 = norm_act(y1, 1)
    o1 = (mxq(h1, 2, "e4m3") @ mxq(f64(w2_l1), 0, "e4m3")) * (1.0 / np.sqrt(F1))
    return np.concatenate([o0, o1.transpose(0, 2, 1).reshape(N, U1 * D1)], axis=1)

@@ -1,0 +1,295 @@
+import math
+from contextlib import ExitStack
+
+import concourse.mybir as mybir
+from concourse.masks import make_identity
+
+F32 = mybir.dt.float32
+BF16 = mybir.dt.bfloat16
+U32 = mybir.dt.uint32
+U8 = mybir.dt.uint8
+FP8X4 = mybir.dt.float8_e4m3fn_x4
+ACT = mybir.ActivationFunctionType
+ALU = mybir.AluOpType
+
+P = 128
+PACK = 4
+N_TOK, U0, U1, F0, F1, D1 = 4096, 512, 128, 1024, 512, 3
+X_COLS = U0 + U1 * D1
+TILES = N_TOK // P
+GROUP = 4
+BATCH = 8
+PASSES0 = F0 // (P * PACK)
+BANK = 512
+
+SCALE_Y0 = 1.0 / math.sqrt(U0)
+SCALE_O0 = 1.0 / math.sqrt(F0)
+SCALE_Y1 = 1.0 / math.sqrt(U1)
+SCALE_O1 = 1.0 / math.sqrt(F1)
+
+FLOPS = 2 * N_TOK * (U0 * F0 + F0 * U0 + D1 * U1 * F1 + D1 * F1 * U1)
+
+
+def tile_intermodule_pa_t_kernel(tc, x, w1_l0, w1_l1, w2_l0, w2_l1, out):
+    nc = tc.nc
+    x_groups = x.rearrange("(g p a) c -> g p a c", p=P, a=GROUP)
+    out_groups = out.rearrange("(g p a) c -> g p a c", p=P, a=GROUP)
+
+    with ExitStack() as pools:
+        const = pools.enter_context(tc.tile_pool(name="const", bufs=1))
+        stage = pools.enter_context(tc.tile_pool(name="stage", bufs=1))
+        x_pool = pools.enter_context(tc.tile_pool(name="x_pool", bufs=3))
+        xt_pool = pools.enter_context(tc.tile_pool(name="xt_pool", bufs=2))
+        ys_pool = pools.enter_context(tc.tile_pool(name="ys_pool", bufs=BATCH + 4))
+        sq_pool = pools.enter_context(tc.tile_pool(name="sq_pool", bufs=2))
+        norm_pool = pools.enter_context(tc.tile_pool(name="norm_pool", bufs=BATCH + 4))
+        h_pool = pools.enter_context(tc.tile_pool(name="h_pool", bufs=2))
+        o_pool = pools.enter_context(tc.tile_pool(name="o_pool", bufs=3))
+        ps_x0 = pools.enter_context(tc.psum_pool(name="ps_x0", bufs=1))
+        ps_x1 = pools.enter_context(tc.psum_pool(name="ps_x1", bufs=1))
+        ps_y0 = pools.enter_context(tc.psum_pool(name="ps_y0", bufs=2))
+        ps_y1 = pools.enter_context(tc.psum_pool(name="ps_y1", bufs=2))
+        ps_o0 = pools.enter_context(tc.psum_pool(name="ps_o0", bufs=1))
+        ps_o1 = pools.enter_context(tc.psum_pool(name="ps_o1", bufs=1))
+
+        x_tiles = {}
+        x1t_tiles = {}
+        x0_codes = {}
+        ys_tiles = {}
+        norm_tiles = {}
+
+        def load_group(g):
+            xg = x_pool.tile([P, GROUP, X_COLS], BF16, name="xg")
+            nc.sync.dma_start(out=xg[:], in_=x_groups[g])
+            x_tiles[g] = xg
+
+        load_group(0)
+        w1l1_raw = stage.tile([P, F1], BF16, name="w1l1_raw")
+        nc.sync.dma_start(out=w1l1_raw[:], in_=w1_l1)
+        w1_raw = stage.tile([P, PACK, F0], BF16, name="w1_raw")
+        for u in range(2):
+            nc.sync.dma_start(
+                out=w1_raw[:, 2 * u : 2 * u + 2, :],
+                in_=w1_l0[256 * u : 256 * (u + 1), :].rearrange("(p e) f -> p e f", e=2),
+            )
+        w2_raw = stage.tile([P, PASSES0, PACK, U0], BF16, name="w2_raw")
+        nc.sync.dma_start(
+            out=w2_raw[:], in_=w2_l0.rearrange("(g p j) n -> p g j n", g=PASSES0, j=PACK)
+        )
+        w3_raw = stage.tile([P, PACK, U1], BF16, name="w3_raw")
+        nc.sync.dma_start(out=w3_raw[:], in_=w2_l1.rearrange("(p j) w -> p j w", j=PACK))
+        load_group(1)
+
+        ident_f32 = const.tile([P, P], F32, name="ident_f32")
+        make_identity(nc, ident_f32[:])
+        ident_bf16 = const.tile([P, P], BF16, name="ident_bf16")
+        make_identity(nc, ident_bf16[:])
+
+        w1l1 = const.tile([P, PACK, P], BF16, name="w1l1")
+        nc.vector.tensor_copy(out=w1l1[:], in_=w1l1_raw[:].rearrange("p (q j) -> p j q", j=PACK))
+
+        w1_grouped = stage.tile([P, F0, PACK], BF16, name="w1_grouped", align_bytes=64)
+        for g in range(PASSES0):
+            nc.scalar.copy(
+                out=w1_grouped[:, BANK * g : BANK * (g + 1), :].rearrange(
+                    "p (j q) t -> p j q t", j=PACK
+                ),
+                in_=w1_raw[:, :, BANK * g : BANK * (g + 1)].rearrange(
+                    "p t (q j) -> p j q t", j=PACK
+                ),
+            )
+        w1_words = const.tile([P, F0], U32, name="w1_words", align_bytes=64)
+        w1_scales = const.tile([P, F0], U8, name="w1_scales", align_bytes=64)
+        nc.vector.quantize_mx(
+            out=w1_words[:].bitcast(FP8X4),
+            scales=w1_scales[:],
+            in_=w1_grouped[:].rearrange("p f t -> p (f t)"),
+        )
+
+        w2_grouped = stage.tile([P, PASSES0, U0, PACK], BF16, name="w2_grouped", align_bytes=64)
+        for g in range(PASSES0):
+            nc.scalar.copy(out=w2_grouped[:, g], in_=w2_raw[:, g].rearrange("p j n -> p n j"))
+        w2_words = const.tile([P, PASSES0 * U0], U32, name="w2_words", align_bytes=64)
+        w2_scales = const.tile([P, PASSES0 * U0], U8, name="w2_scales", align_bytes=64)
+        nc.vector.quantize_mx(
+            out=w2_words[:].bitcast(FP8X4),
+            scales=w2_scales[:],
+            in_=w2_grouped[:].rearrange("p g n j -> p (g n j)"),
+        )
+
+        w3_grouped = stage.tile([P, U1, PACK], BF16, name="w3_grouped", align_bytes=64)
+        nc.vector.tensor_copy(out=w3_grouped[:], in_=w3_raw[:].rearrange("p j w -> p w j"))
+        w3_words = const.tile([P, U1], U32, name="w3_words", align_bytes=64)
+        w3_scales = const.tile([P, U1], U8, name="w3_scales", align_bytes=64)
+        nc.vector.quantize_mx(
+            out=w3_words[:].bitcast(FP8X4),
+            scales=w3_scales[:],
+            in_=w3_grouped[:].rearrange("p w j -> p (w j)"),
+        )
+
+        def transpose_pair(pair):
+            xg = x_tiles[pair // 2]
+            x_as_words = xg[:].rearrange("p a c -> p (a c)").bitcast(F32)
+            x0_t = ps_x0.tile([P, 2, 2, P], F32, name="x0_t")
+            x1_t = ps_x1.tile([P, 2, D1, P], BF16, name="x1_t")
+            for half in range(2):
+                a = 2 * (pair % 2) + half
+                first_word = a * (X_COLS // 2)
+                for u in range(2):
+                    nc.tensor.transpose(
+                        x0_t[:, half, u, :],
+                        x_as_words[:, first_word + P * u : first_word + P * (u + 1)],
+                        ident_f32[:],
+                    )
+                for c in range(D1):
+                    nc.tensor.transpose(
+                        x1_t[:, half, c, :], xg[:, a, U0 + c : X_COLS : D1], ident_bf16[:]
+                    )
+            x0_grouped = xt_pool.tile([P, 2 * P * PACK], BF16, name="x0_grouped", align_bytes=64)
+            nc.vector.tensor_copy(
+                out=x0_grouped[:].bitcast(F32).rearrange("p (h t u) -> p h t u", h=2, u=2),
+                in_=x0_t[:].rearrange("p h u t -> p h t u"),
+            )
+            x1t = xt_pool.tile([P, 2, D1, P], BF16, name="x1t")
+            nc.vector.tensor_copy(out=x1t[:], in_=x1_t[:])
+            words = xt_pool.tile([P, 2 * P], U32, name="x0_words", align_bytes=64)
+            scales = xt_pool.tile([P, 2 * P], U8, name="x0_scales", align_bytes=64)
+            nc.vector.quantize_mx(
+                out=words[:].bitcast(FP8X4), scales=scales[:], in_=x0_grouped[:]
+            )
+            x1t_tiles[pair] = x1t
+            x0_codes[pair] = (words, scales)
+
+        def vector_front(i):
+            x1t = x1t_tiles[i // 2]
+            ys = ys_pool.tile([P, D1, BANK], F32, name="ys")
+            for c in range(D1):
+                y1 = ps_y1.tile([P, PACK, P], F32, name="y1")
+                for j in range(PACK):
+                    nc.tensor.matmul(
+                        y1[:, j, :], lhsT=w1l1[:, j, :], rhs=x1t[:, i % 2, c, :],
+                        start=True, stop=True,
+                    )
+                nc.vector.tensor_scalar_mul(
+                    out=ys[:, c, :].rearrange("p (t j) -> p t j", j=PACK),
+                    in0=y1[:].rearrange("p j t -> p t j"),
+                    scalar1=SCALE_Y1,
+                )
+            ys_tiles[i] = ys
+            sq = sq_pool.tile([P, D1, BANK], F32, name="sq")
+            nc.scalar.activation(out=sq[:], in_=ys[:], func=ACT.Square)
+            norm = norm_pool.tile([P, BANK], F32, name="norm")
+            nc.gpsimd.tensor_tensor(out=norm[:], in0=sq[:, 0, :], in1=sq[:, 1, :], op=ALU.add)
+            nc.gpsimd.tensor_tensor(out=norm[:], in0=norm[:], in1=sq[:, 2, :], op=ALU.add)
+            norm_tiles[i] = norm
+
+        def batch_roots(b):
+            for i in range(BATCH * b, BATCH * (b + 1)):
+                norm = norm_tiles[i]
+                nc.scalar.activation(out=norm[:], in_=norm[:], func=ACT.Sqrt)
+
+        def vector_back(i):
+            ys = ys_tiles[i]
+            norm = norm_tiles[i]
+            nc.scalar.activation(out=norm[:], in_=norm[:], func=ACT.Sigmoid)
+            h1 = h_pool.tile([P, D1, BANK], BF16, name="h1", align_bytes=64)
+            nc.gpsimd.tensor_tensor(
+                out=h1[:], in0=ys[:], in1=norm[:].unsqueeze(1).to_broadcast([P, D1, BANK]),
+                op=ALU.mult,
+            )
+            words = h_pool.tile([P, D1, P], U32, name="h1_words", align_bytes=64)
+            scales = h_pool.tile([P, D1, P], U8, name="h1_scales", align_bytes=64)
+            for c in range(D1):
+                nc.vector.quantize_mx(
+                    out=words[:, c, :].bitcast(FP8X4), scales=scales[:, c, :], in_=h1[:, c, :]
+                )
+            o1_ps = ps_o1.tile([P, D1, U1], F32, name="o1_ps")
+            for c in range(D1):
+                nc.tensor.matmul_mx(
+                    out=o1_ps[:, c, :],
+                    lhsT=words[:, c, :].bitcast(FP8X4),
+                    lhsT_scale=scales[:, c, :],
+                    rhs=w3_words[:].bitcast(FP8X4),
+                    rhs_scale=w3_scales[:],
+                    start=True,
+                    stop=True,
+                )
+            o1 = o_pool.tile([P, U1 * D1], F32, name="o1")
+            nc.vector.tensor_scalar_mul(
+                out=o1[:].rearrange("p (w c) -> p w c", c=D1),
+                in0=o1_ps[:].rearrange("p c w -> p w c"),
+                scalar1=SCALE_O1,
+            )
+            nc.sync.dma_start(out=out_groups[i // GROUP][:, i % GROUP, U0:X_COLS], in_=o1[:])
+
+        def scalar_path(i):
+            x_words, x_scales = x0_codes[i // 2]
+            tokens = slice(P * (i % 2), P * (i % 2 + 1))
+            sig0 = h_pool.tile([P, PASSES0, BANK], F32, name="sig0")
+            y0_banks = []
+            for g in range(PASSES0):
+                y0 = ps_y0.tile([P, PACK, P], F32, name="y0")
+                for j in range(PACK):
+                    chunk = slice(P * (PACK * g + j), P * (PACK * g + j + 1))
+                    nc.tensor.matmul_mx(
+                        out=y0[:, j, :],
+                        lhsT=w1_words[:, chunk].bitcast(FP8X4),
+                        lhsT_scale=w1_scales[:, chunk],
+                        rhs=x_words[:, tokens].bitcast(FP8X4),
+                        rhs_scale=x_scales[:, tokens],
+                        start=True,
+                        stop=True,
+                    )
+                nc.scalar.activation(
+                    out=sig0[:, g, :].rearrange("p (t j) -> p t j", j=PACK),
+                    in_=y0[:].rearrange("p j t -> p t j"),
+                    func=ACT.Abs,
+                    scale=SCALE_Y0,
+                )
+                y0_banks.append(y0)
+            nc.scalar.activation(out=sig0[:], in_=sig0[:], func=ACT.Sigmoid)
+            h0 = h_pool.tile([P, PASSES0, BANK], BF16, name="h0", align_bytes=64)
+            for g in range(PASSES0):
+                nc.vector.scalar_tensor_tensor(
+                    out=h0[:, g, :].rearrange("p (t j) -> p t j", j=PACK),
+                    in0=y0_banks[g][:].rearrange("p j t -> p t j"),
+                    scalar=SCALE_Y0,
+                    in1=sig0[:, g, :].rearrange("p (t j) -> p t j", j=PACK),
+                    op0=ALU.mult,
+                    op1=ALU.mult,
+                )
+            words = h_pool.tile([P, PASSES0, P], U32, name="h0_words", align_bytes=64)
+            scales = h_pool.tile([P, PASSES0, P], U8, name="h0_scales", align_bytes=64)
+            nc.vector.quantize_mx(
+                out=words[:].rearrange("p g t -> p (g t)").bitcast(FP8X4),
+                scales=scales[:].rearrange("p g t -> p (g t)"),
+                in_=h0[:].rearrange("p g c -> p (g c)"),
+            )
+            o0_ps = ps_o0.tile([P, U0], F32, name="o0_ps")
+            for g in range(PASSES0):
+                nc.tensor.matmul_mx(
+                    out=o0_ps[:],
+                    lhsT=words[:, g, :].bitcast(FP8X4),
+                    lhsT_scale=scales[:, g, :],
+                    rhs=w2_words[:, U0 * g : U0 * (g + 1)].bitcast(FP8X4),
+                    rhs_scale=w2_scales[:, U0 * g : U0 * (g + 1)],
+                    start=(g == 0),
+                    stop=(g == PASSES0 - 1),
+                )
+            o0 = o_pool.tile([P, U0], F32, name="o0")
+            nc.vector.tensor_scalar_mul(out=o0[:], in0=o0_ps[:], scalar1=SCALE_O0)
+            nc.sync.dma_start(out=out_groups[i // GROUP][:, i % GROUP, 0:U0], in_=o0[:])
+
+        LAG = BATCH + 2
+        for step in range(TILES + LAG):
+            if step < TILES:
+                if step % GROUP == 0 and step // GROUP + 2 < TILES // GROUP:
+                    load_group(step // GROUP + 2)
+                if step % 2 == 0:
+                    transpose_pair(step // 2)
+                vector_front(step)
+                scalar_path(step)
+            if step >= LAG:
+                if (step - LAG) % BATCH == 0:
+                    batch_roots((step - LAG) // BATCH)
+                vector_back(step - LAG)

@@ -21,6 +21,7 @@ GROUP = 4
 BATCH = 8
 PASSES0 = F0 // (P * PACK)
 BANK = 512
+LAG = BATCH + 3
 
 SCALE_Y0 = 1.0 / math.sqrt(U0)
 SCALE_O0 = 1.0 / math.sqrt(F0)
@@ -39,24 +40,26 @@ def tile_intermodule_pa_t_kernel(tc, x, w1_l0, w1_l1, w2_l0, w2_l1, out):
         const = pools.enter_context(tc.tile_pool(name="const", bufs=1))
         stage = pools.enter_context(tc.tile_pool(name="stage", bufs=1))
         x_pool = pools.enter_context(tc.tile_pool(name="x_pool", bufs=3))
-        xt_pool = pools.enter_context(tc.tile_pool(name="xt_pool", bufs=2))
-        ys_pool = pools.enter_context(tc.tile_pool(name="ys_pool", bufs=BATCH + 4))
-        sq_pool = pools.enter_context(tc.tile_pool(name="sq_pool", bufs=2))
-        norm_pool = pools.enter_context(tc.tile_pool(name="norm_pool", bufs=BATCH + 4))
-        h_pool = pools.enter_context(tc.tile_pool(name="h_pool", bufs=2))
-        o_pool = pools.enter_context(tc.tile_pool(name="o_pool", bufs=3))
-        ps_x0 = pools.enter_context(tc.psum_pool(name="ps_x0", bufs=1))
-        ps_x1 = pools.enter_context(tc.psum_pool(name="ps_x1", bufs=1))
-        ps_y0 = pools.enter_context(tc.psum_pool(name="ps_y0", bufs=2))
-        ps_y1 = pools.enter_context(tc.psum_pool(name="ps_y1", bufs=2))
-        ps_o0 = pools.enter_context(tc.psum_pool(name="ps_o0", bufs=1))
-        ps_o1 = pools.enter_context(tc.psum_pool(name="ps_o1", bufs=1))
+        short = pools.enter_context(tc.tile_pool(name="short", bufs=2))
+        waiting = pools.enter_context(tc.tile_pool(name="waiting", bufs=LAG + 1))
+        o_pool = pools.enter_context(tc.tile_pool(name="o_pool", bufs=4))
+        ps_y0 = pools.enter_context(tc.psum_pool(name="ps_y0", bufs=2 * PASSES0))
+        ring = pools.enter_context(tc.psum_pool(name="ring", bufs=4))
 
         x_tiles = {}
         x1t_tiles = {}
+        x0_grouped_tiles = {}
         x0_codes = {}
         ys_tiles = {}
+        sq_tiles = {}
         norm_tiles = {}
+        y0_tiles = {}
+        sig0_tiles = {}
+        h0_tiles = {}
+        h0_codes = {}
+        h1_tiles = {}
+        h1_codes = {}
+        out_tiles = {}
 
         def load_group(g):
             xg = x_pool.tile([P, GROUP, X_COLS], BF16, name="xg")
@@ -66,6 +69,7 @@ def tile_intermodule_pa_t_kernel(tc, x, w1_l0, w1_l1, w2_l0, w2_l1, out):
         load_group(0)
         w1l1_raw = stage.tile([P, F1], BF16, name="w1l1_raw")
         nc.sync.dma_start(out=w1l1_raw[:], in_=w1_l1)
+        load_group(1)
         w1_raw = stage.tile([P, PACK, F0], BF16, name="w1_raw")
         for u in range(2):
             nc.sync.dma_start(
@@ -78,7 +82,6 @@ def tile_intermodule_pa_t_kernel(tc, x, w1_l0, w1_l1, w2_l0, w2_l1, out):
         )
         w3_raw = stage.tile([P, PACK, U1], BF16, name="w3_raw")
         nc.sync.dma_start(out=w3_raw[:], in_=w2_l1.rearrange("(p j) w -> p j w", j=PACK))
-        load_group(1)
 
         ident_f32 = const.tile([P, P], F32, name="ident_f32")
         make_identity(nc, ident_f32[:])
@@ -89,7 +92,16 @@ def tile_intermodule_pa_t_kernel(tc, x, w1_l0, w1_l1, w2_l0, w2_l1, out):
         nc.vector.tensor_copy(out=w1l1[:], in_=w1l1_raw[:].rearrange("p (q j) -> p j q", j=PACK))
 
         w1_grouped = stage.tile([P, F0, PACK], BF16, name="w1_grouped", align_bytes=64)
-        for g in range(PASSES0):
+        w2_grouped = stage.tile([P, PASSES0, U0, PACK], BF16, name="w2_grouped", align_bytes=64)
+        w3_grouped = stage.tile([P, U1, PACK], BF16, name="w3_grouped", align_bytes=64)
+        w1_words = const.tile([P, F0], U32, name="w1_words", align_bytes=64)
+        w1_scales = const.tile([P, F0], U8, name="w1_scales", align_bytes=64)
+        w2_words = const.tile([P, PASSES0 * U0], U32, name="w2_words", align_bytes=64)
+        w2_scales = const.tile([P, PASSES0 * U0], U8, name="w2_scales", align_bytes=64)
+        w3_words = const.tile([P, U1], U32, name="w3_words", align_bytes=64)
+        w3_scales = const.tile([P, U1], U8, name="w3_scales", align_bytes=64)
+
+        def regroup_w1(g):
             nc.scalar.copy(
                 out=w1_grouped[:, BANK * g : BANK * (g + 1), :].rearrange(
                     "p (j q) t -> p j q t", j=PACK
@@ -98,87 +110,89 @@ def tile_intermodule_pa_t_kernel(tc, x, w1_l0, w1_l1, w2_l0, w2_l1, out):
                     "p t (q j) -> p j q t", j=PACK
                 ),
             )
-        w1_words = const.tile([P, F0], U32, name="w1_words", align_bytes=64)
-        w1_scales = const.tile([P, F0], U8, name="w1_scales", align_bytes=64)
-        nc.vector.quantize_mx(
-            out=w1_words[:].bitcast(FP8X4),
-            scales=w1_scales[:],
-            in_=w1_grouped[:].rearrange("p f t -> p (f t)"),
-        )
 
-        w2_grouped = stage.tile([P, PASSES0, U0, PACK], BF16, name="w2_grouped", align_bytes=64)
-        for g in range(PASSES0):
+        def regroup_w2(g):
             nc.scalar.copy(out=w2_grouped[:, g], in_=w2_raw[:, g].rearrange("p j n -> p n j"))
-        w2_words = const.tile([P, PASSES0 * U0], U32, name="w2_words", align_bytes=64)
-        w2_scales = const.tile([P, PASSES0 * U0], U8, name="w2_scales", align_bytes=64)
-        nc.vector.quantize_mx(
-            out=w2_words[:].bitcast(FP8X4),
-            scales=w2_scales[:],
-            in_=w2_grouped[:].rearrange("p g n j -> p (g n j)"),
-        )
 
-        w3_grouped = stage.tile([P, U1, PACK], BF16, name="w3_grouped", align_bytes=64)
-        nc.vector.tensor_copy(out=w3_grouped[:], in_=w3_raw[:].rearrange("p j w -> p w j"))
-        w3_words = const.tile([P, U1], U32, name="w3_words", align_bytes=64)
-        w3_scales = const.tile([P, U1], U8, name="w3_scales", align_bytes=64)
-        nc.vector.quantize_mx(
-            out=w3_words[:].bitcast(FP8X4),
-            scales=w3_scales[:],
-            in_=w3_grouped[:].rearrange("p w j -> p (w j)"),
-        )
-
-        def transpose_pair(pair):
-            xg = x_tiles[pair // 2]
-            x_as_words = xg[:].rearrange("p a c -> p (a c)").bitcast(F32)
-            x0_t = ps_x0.tile([P, 2, 2, P], F32, name="x0_t")
-            x1_t = ps_x1.tile([P, 2, D1, P], BF16, name="x1_t")
-            for half in range(2):
-                a = 2 * (pair % 2) + half
-                first_word = a * (X_COLS // 2)
-                for u in range(2):
-                    nc.tensor.transpose(
-                        x0_t[:, half, u, :],
-                        x_as_words[:, first_word + P * u : first_word + P * (u + 1)],
-                        ident_f32[:],
-                    )
-                for c in range(D1):
-                    nc.tensor.transpose(
-                        x1_t[:, half, c, :], xg[:, a, U0 + c : X_COLS : D1], ident_bf16[:]
-                    )
-            x0_grouped = xt_pool.tile([P, 2 * P * PACK], BF16, name="x0_grouped", align_bytes=64)
-            nc.vector.tensor_copy(
-                out=x0_grouped[:].bitcast(F32).rearrange("p (h t u) -> p h t u", h=2, u=2),
-                in_=x0_t[:].rearrange("p h u t -> p h t u"),
-            )
-            x1t = xt_pool.tile([P, 2, D1, P], BF16, name="x1t")
-            nc.vector.tensor_copy(out=x1t[:], in_=x1_t[:])
-            words = xt_pool.tile([P, 2 * P], U32, name="x0_words", align_bytes=64)
-            scales = xt_pool.tile([P, 2 * P], U8, name="x0_scales", align_bytes=64)
+        def quantise_weights():
+            nc.vector.tensor_copy(out=w3_grouped[:], in_=w3_raw[:].rearrange("p j w -> p w j"))
             nc.vector.quantize_mx(
-                out=words[:].bitcast(FP8X4), scales=scales[:], in_=x0_grouped[:]
+                out=w1_words[:].bitcast(FP8X4),
+                scales=w1_scales[:],
+                in_=w1_grouped[:].rearrange("p f t -> p (f t)"),
             )
-            x1t_tiles[pair] = x1t
-            x0_codes[pair] = (words, scales)
+            nc.vector.quantize_mx(
+                out=w2_words[:].bitcast(FP8X4),
+                scales=w2_scales[:],
+                in_=w2_grouped[:].rearrange("p g n j -> p (g n j)"),
+            )
+            nc.vector.quantize_mx(
+                out=w3_words[:].bitcast(FP8X4),
+                scales=w3_scales[:],
+                in_=w3_grouped[:].rearrange("p w j -> p (w j)"),
+            )
 
-        def vector_front(i):
-            x1t = x1t_tiles[i // 2]
-            ys = ys_pool.tile([P, D1, BANK], F32, name="ys")
-            for c in range(D1):
-                y1 = ps_y1.tile([P, PACK, P], F32, name="y1")
-                for j in range(PACK):
-                    nc.tensor.matmul(
-                        y1[:, j, :], lhsT=w1l1[:, j, :], rhs=x1t[:, i % 2, c, :],
-                        start=True, stop=True,
-                    )
-                nc.vector.tensor_scalar_mul(
-                    out=ys[:, c, :].rearrange("p (t j) -> p t j", j=PACK),
-                    in0=y1[:].rearrange("p j t -> p t j"),
-                    scalar1=SCALE_Y1,
+        def transpose_x(i):
+            xg = x_tiles[i // GROUP]
+            a = i % GROUP
+            x_as_words = xg[:].rearrange("p a c -> p (a c)").bitcast(F32)
+            first_word = a * (X_COLS // 2)
+            xt = ring.tile([P, BANK], F32, name="xt", tag="ring")
+            x0_t = xt[:, 0 : 2 * P].rearrange("p (u t) -> p u t", u=2)
+            x1_t = xt[:, 2 * P : 2 * P + D1 * P // 2].bitcast(BF16).rearrange(
+                "p (c t) -> p c t", c=D1
+            )
+            for u in range(2):
+                nc.tensor.transpose(
+                    x0_t[:, u, :],
+                    x_as_words[:, first_word + P * u : first_word + P * (u + 1)],
+                    ident_f32[:],
                 )
-            ys_tiles[i] = ys
-            sq = sq_pool.tile([P, D1, BANK], F32, name="sq")
-            nc.scalar.activation(out=sq[:], in_=ys[:], func=ACT.Square)
-            norm = norm_pool.tile([P, BANK], F32, name="norm")
+            for c in range(D1):
+                nc.tensor.transpose(
+                    x1_t[:, c, :], xg[:, a, U0 + c : X_COLS : D1], ident_bf16[:]
+                )
+            x0_grouped = short.tile([P, P * PACK], BF16, name="x0_grouped", align_bytes=64)
+            nc.vector.tensor_copy(
+                out=x0_grouped[:].bitcast(F32).rearrange("p (t u) -> p t u", u=2),
+                in_=x0_t.rearrange("p u t -> p t u"),
+            )
+            x1t = short.tile([P, D1, P], BF16, name="x1t")
+            nc.vector.tensor_copy(out=x1t[:], in_=x1_t)
+            x0_grouped_tiles[i] = x0_grouped
+            x1t_tiles[i] = x1t
+
+        def quantise_x0(i):
+            words = waiting.tile([P, P], U32, name="x0_words", align_bytes=64)
+            scales = waiting.tile([P, P], U8, name="x0_scales", align_bytes=64)
+            nc.vector.quantize_mx(
+                out=words[:].bitcast(FP8X4), scales=scales[:], in_=x0_grouped_tiles[i][:]
+            )
+            x0_codes[i] = (words, scales)
+
+        def y1_component(i, c):
+            if c == 0:
+                ys_tiles[i] = waiting.tile([P, D1, BANK], F32, name="ys")
+            y1 = ring.tile([P, PACK, P], F32, name="y1", tag="ring")
+            for j in range(PACK):
+                nc.tensor.matmul(
+                    y1[:, j, :], lhsT=w1l1[:, j, :], rhs=x1t_tiles[i][:, c, :],
+                    start=True, stop=True,
+                )
+            nc.vector.tensor_scalar_mul(
+                out=ys_tiles[i][:, c, :].rearrange("p (t j) -> p t j", j=PACK),
+                in0=y1[:].rearrange("p j t -> p t j"),
+                scalar1=SCALE_Y1,
+            )
+
+        def square_y1(i):
+            sq = short.tile([P, D1, BANK], F32, name="sq")
+            nc.scalar.activation(out=sq[:], in_=ys_tiles[i][:], func=ACT.Square)
+            sq_tiles[i] = sq
+
+        def add_squares(i):
+            sq = sq_tiles[i]
+            norm = waiting.tile([P, BANK], F32, name="norm")
             nc.gpsimd.tensor_tensor(out=norm[:], in0=sq[:, 0, :], in1=sq[:, 1, :], op=ALU.add)
             nc.gpsimd.tensor_tensor(out=norm[:], in0=norm[:], in1=sq[:, 2, :], op=ALU.add)
             norm_tiles[i] = norm
@@ -188,22 +202,34 @@ def tile_intermodule_pa_t_kernel(tc, x, w1_l0, w1_l1, w2_l0, w2_l1, out):
                 norm = norm_tiles[i]
                 nc.scalar.activation(out=norm[:], in_=norm[:], func=ACT.Sqrt)
 
-        def vector_back(i):
-            ys = ys_tiles[i]
+        def sigmoid_norm(i):
             norm = norm_tiles[i]
             nc.scalar.activation(out=norm[:], in_=norm[:], func=ACT.Sigmoid)
-            h1 = h_pool.tile([P, D1, BANK], BF16, name="h1", align_bytes=64)
+
+        def gate_y1(i):
+            h1 = short.tile([P, D1, BANK], BF16, name="h1", align_bytes=64)
             nc.gpsimd.tensor_tensor(
-                out=h1[:], in0=ys[:], in1=norm[:].unsqueeze(1).to_broadcast([P, D1, BANK]),
+                out=h1[:],
+                in0=ys_tiles[i][:],
+                in1=norm_tiles[i][:].unsqueeze(1).to_broadcast([P, D1, BANK]),
                 op=ALU.mult,
             )
-            words = h_pool.tile([P, D1, P], U32, name="h1_words", align_bytes=64)
-            scales = h_pool.tile([P, D1, P], U8, name="h1_scales", align_bytes=64)
+            h1_tiles[i] = h1
+
+        def quantise_h1(i):
+            words = short.tile([P, D1, P], U32, name="h1_words", align_bytes=64)
+            scales = short.tile([P, D1, P], U8, name="h1_scales", align_bytes=64)
             for c in range(D1):
                 nc.vector.quantize_mx(
-                    out=words[:, c, :].bitcast(FP8X4), scales=scales[:, c, :], in_=h1[:, c, :]
+                    out=words[:, c, :].bitcast(FP8X4),
+                    scales=scales[:, c, :],
+                    in_=h1_tiles[i][:, c, :],
                 )
-            o1_ps = ps_o1.tile([P, D1, U1], F32, name="o1_ps")
+            h1_codes[i] = (words, scales)
+
+        def second_vector_matmul(i):
+            words, scales = h1_codes[i]
+            o1_ps = ring.tile([P, D1, U1], F32, name="o1_ps", tag="ring")
             for c in range(D1):
                 nc.tensor.matmul_mx(
                     out=o1_ps[:, c, :],
@@ -214,19 +240,15 @@ def tile_intermodule_pa_t_kernel(tc, x, w1_l0, w1_l1, w2_l0, w2_l1, out):
                     start=True,
                     stop=True,
                 )
-            o1 = o_pool.tile([P, U1 * D1], F32, name="o1")
             nc.vector.tensor_scalar_mul(
-                out=o1[:].rearrange("p (w c) -> p w c", c=D1),
+                out=out_tiles[i][:, U0:X_COLS].rearrange("p (w c) -> p w c", c=D1),
                 in0=o1_ps[:].rearrange("p c w -> p w c"),
                 scalar1=SCALE_O1,
             )
-            nc.sync.dma_start(out=out_groups[i // GROUP][:, i % GROUP, U0:X_COLS], in_=o1[:])
 
-        def scalar_path(i):
-            x_words, x_scales = x0_codes[i // 2]
-            tokens = slice(P * (i % 2), P * (i % 2 + 1))
-            sig0 = h_pool.tile([P, PASSES0, BANK], F32, name="sig0")
-            y0_banks = []
+        def first_scalar_matmul(i):
+            x_words, x_scales = x0_codes[i]
+            y0_tiles[i] = []
             for g in range(PASSES0):
                 y0 = ps_y0.tile([P, PACK, P], F32, name="y0")
                 for j in range(PACK):
@@ -235,37 +257,51 @@ def tile_intermodule_pa_t_kernel(tc, x, w1_l0, w1_l1, w2_l0, w2_l1, out):
                         out=y0[:, j, :],
                         lhsT=w1_words[:, chunk].bitcast(FP8X4),
                         lhsT_scale=w1_scales[:, chunk],
-                        rhs=x_words[:, tokens].bitcast(FP8X4),
-                        rhs_scale=x_scales[:, tokens],
+                        rhs=x_words[:].bitcast(FP8X4),
+                        rhs_scale=x_scales[:],
                         start=True,
                         stop=True,
                     )
+                y0_tiles[i].append(y0)
+
+        def sigmoid_abs_y0(i):
+            sig0 = short.tile([P, PASSES0, BANK], F32, name="sig0")
+            for g in range(PASSES0):
                 nc.scalar.activation(
                     out=sig0[:, g, :].rearrange("p (t j) -> p t j", j=PACK),
-                    in_=y0[:].rearrange("p j t -> p t j"),
+                    in_=y0_tiles[i][g][:].rearrange("p j t -> p t j"),
                     func=ACT.Abs,
                     scale=SCALE_Y0,
                 )
-                y0_banks.append(y0)
             nc.scalar.activation(out=sig0[:], in_=sig0[:], func=ACT.Sigmoid)
-            h0 = h_pool.tile([P, PASSES0, BANK], BF16, name="h0", align_bytes=64)
+            sig0_tiles[i] = sig0
+
+        def gate_y0(i):
+            h0 = short.tile([P, PASSES0, BANK], BF16, name="h0", align_bytes=64)
             for g in range(PASSES0):
                 nc.vector.scalar_tensor_tensor(
                     out=h0[:, g, :].rearrange("p (t j) -> p t j", j=PACK),
-                    in0=y0_banks[g][:].rearrange("p j t -> p t j"),
+                    in0=y0_tiles[i][g][:].rearrange("p j t -> p t j"),
                     scalar=SCALE_Y0,
-                    in1=sig0[:, g, :].rearrange("p (t j) -> p t j", j=PACK),
+                    in1=sig0_tiles[i][:, g, :].rearrange("p (t j) -> p t j", j=PACK),
                     op0=ALU.mult,
                     op1=ALU.mult,
                 )
-            words = h_pool.tile([P, PASSES0, P], U32, name="h0_words", align_bytes=64)
-            scales = h_pool.tile([P, PASSES0, P], U8, name="h0_scales", align_bytes=64)
+            h0_tiles[i] = h0
+
+        def quantise_h0(i):
+            words = short.tile([P, PASSES0, P], U32, name="h0_words", align_bytes=64)
+            scales = short.tile([P, PASSES0, P], U8, name="h0_scales", align_bytes=64)
             nc.vector.quantize_mx(
                 out=words[:].rearrange("p g t -> p (g t)").bitcast(FP8X4),
                 scales=scales[:].rearrange("p g t -> p (g t)"),
-                in_=h0[:].rearrange("p g c -> p (g c)"),
+                in_=h0_tiles[i][:].rearrange("p g c -> p (g c)"),
             )
-            o0_ps = ps_o0.tile([P, U0], F32, name="o0_ps")
+            h0_codes[i] = (words, scales)
+
+        def second_scalar_matmul(i):
+            words, scales = h0_codes[i]
+            o0_ps = ring.tile([P, U0], F32, name="o0_ps", tag="ring")
             for g in range(PASSES0):
                 nc.tensor.matmul_mx(
                     out=o0_ps[:],
@@ -276,20 +312,59 @@ def tile_intermodule_pa_t_kernel(tc, x, w1_l0, w1_l1, w2_l0, w2_l1, out):
                     start=(g == 0),
                     stop=(g == PASSES0 - 1),
                 )
-            o0 = o_pool.tile([P, U0], F32, name="o0")
-            nc.vector.tensor_scalar_mul(out=o0[:], in0=o0_ps[:], scalar1=SCALE_O0)
-            nc.sync.dma_start(out=out_groups[i // GROUP][:, i % GROUP, 0:U0], in_=o0[:])
+            out_tiles[i] = o_pool.tile([P, X_COLS], F32, name="out_tile")
+            nc.vector.tensor_scalar_mul(
+                out=out_tiles[i][:, 0:U0], in0=o0_ps[:], scalar1=SCALE_O0
+            )
 
-        LAG = BATCH + 2
-        for step in range(TILES + LAG):
-            if step < TILES:
-                if step % GROUP == 0 and step // GROUP + 2 < TILES // GROUP:
-                    load_group(step // GROUP + 2)
-                if step % 2 == 0:
-                    transpose_pair(step // 2)
-                vector_front(step)
-                scalar_path(step)
-            if step >= LAG:
-                if (step - LAG) % BATCH == 0:
-                    batch_roots((step - LAG) // BATCH)
-                vector_back(step - LAG)
+        def store(i):
+            nc.sync.dma_start(out=out_groups[i // GROUP][:, i % GROUP, :], in_=out_tiles[i][:])
+
+        def is_tile(i):
+            return 0 <= i < TILES
+
+        pools.enter_context(tc.manual_schedule())
+        for step in range(-1, TILES + LAG + 3):
+            front = step
+            back = step - LAG
+            if step % GROUP == 0 and step // GROUP + 2 < TILES // GROUP:
+                load_group(step // GROUP + 2)
+            if is_tile(front + 1):
+                transpose_x(front + 1)
+            if is_tile(front):
+                y1_component(front, 0)
+            if is_tile(front + 1):
+                quantise_x0(front + 1)
+            if is_tile(front):
+                y1_component(front, 1)
+                y1_component(front, 2)
+            if is_tile(back):
+                sigmoid_abs_y0(back)
+            if is_tile(front - 1):
+                square_y1(front - 1)
+            if 0 <= step < PASSES0:
+                regroup_w1(step)
+            if PASSES0 <= step < 2 * PASSES0:
+                regroup_w2(step - PASSES0)
+            if step == 2 * PASSES0:
+                quantise_weights()
+            if is_tile(front - 2):
+                add_squares(front - 2)
+            if is_tile(back + 1) and (back + 1) % BATCH == 0:
+                batch_roots((back + 1) // BATCH)
+            if is_tile(back + 1):
+                sigmoid_norm(back + 1)
+            if is_tile(back):
+                gate_y1(back)
+                gate_y0(back)
+            if is_tile(back - 1):
+                second_scalar_matmul(back - 1)
+            if is_tile(back):
+                quantise_h0(back)
+            if is_tile(back - 1):
+                quantise_h1(back - 1)
+            if is_tile(back - 2):
+                second_vector_matmul(back - 2)
+                store(back - 2)
+            if is_tile(back + 1):
+                first_scalar_matmul(back + 1)

@@ -22,6 +22,7 @@ BATCH = 8
 PASSES0 = F0 // (P * PACK)
 BANK = 512
 LAG = BATCH + 3
+GPSIMD_PARTS = 2
 
 SCALE_Y0 = 1.0 / math.sqrt(U0)
 SCALE_O0 = 1.0 / math.sqrt(F0)
@@ -209,11 +210,15 @@ def tile_intermodule_pa_t_kernel(tc, x, w1_l0, w1_l1, w2_l0, w2_l1, out):
         def gate_y1(i):
             h1 = short.tile([P, D1, BANK], BF16, name="h1", align_bytes=64)
             nc.gpsimd.tensor_tensor(
-                out=h1[:],
-                in0=ys_tiles[i][:],
-                in1=norm_tiles[i][:].unsqueeze(1).to_broadcast([P, D1, BANK]),
+                out=h1[:, 0:GPSIMD_PARTS, :],
+                in0=ys_tiles[i][:, 0:GPSIMD_PARTS, :],
+                in1=norm_tiles[i][:].unsqueeze(1).to_broadcast([P, GPSIMD_PARTS, BANK]),
                 op=ALU.mult,
             )
+            for c in range(GPSIMD_PARTS, D1):
+                nc.vector.tensor_tensor(
+                    out=h1[:, c, :], in0=ys_tiles[i][:, c, :], in1=norm_tiles[i][:], op=ALU.mult
+                )
             h1_tiles[i] = h1
 
         def quantise_h1(i):

@@ -21,8 +21,9 @@ GROUP = 4
 BATCH = 8
 PASSES0 = F0 // (P * PACK)
 BANK = 512
-LAG = BATCH + 3
-GPSIMD_PARTS = 2
+LAG = BATCH + 4
+KEPT = 2
+H_PLANES = PASSES0 + D1
 
 SCALE_Y0 = 1.0 / math.sqrt(U0)
 SCALE_O0 = 1.0 / math.sqrt(F0)
@@ -40,12 +41,13 @@ def tile_intermodule_pa_t_kernel(tc, x, w1_l0, w1_l1, w2_l0, w2_l1, out):
     with ExitStack() as pools:
         const = pools.enter_context(tc.tile_pool(name="const", bufs=1))
         stage = pools.enter_context(tc.tile_pool(name="stage", bufs=1))
-        x_pool = pools.enter_context(tc.tile_pool(name="x_pool", bufs=3))
+        x_pool = pools.enter_context(tc.tile_pool(name="x_pool", bufs=2))
         short = pools.enter_context(tc.tile_pool(name="short", bufs=2))
-        waiting = pools.enter_context(tc.tile_pool(name="waiting", bufs=LAG + 1))
+        waiting = pools.enter_context(tc.tile_pool(name="waiting", bufs=LAG + 2))
         o_pool = pools.enter_context(tc.tile_pool(name="o_pool", bufs=4))
         ps_y0 = pools.enter_context(tc.psum_pool(name="ps_y0", bufs=2 * PASSES0))
-        ring = pools.enter_context(tc.psum_pool(name="ring", bufs=4))
+        ring = pools.enter_context(tc.psum_pool(name="ring", bufs=3))
+        ps_sq = pools.enter_context(tc.psum_pool(name="ps_sq", bufs=1))
 
         x_tiles = {}
         x1t_tiles = {}
@@ -56,10 +58,8 @@ def tile_intermodule_pa_t_kernel(tc, x, w1_l0, w1_l1, w2_l0, w2_l1, out):
         norm_tiles = {}
         y0_tiles = {}
         sig0_tiles = {}
-        h0_tiles = {}
-        h0_codes = {}
-        h1_tiles = {}
-        h1_codes = {}
+        h_tiles = {}
+        h_codes = {}
         out_tiles = {}
 
         def load_group(g):
@@ -70,7 +70,6 @@ def tile_intermodule_pa_t_kernel(tc, x, w1_l0, w1_l1, w2_l0, w2_l1, out):
         load_group(0)
         w1l1_raw = stage.tile([P, F1], BF16, name="w1l1_raw")
         nc.sync.dma_start(out=w1l1_raw[:], in_=w1_l1)
-        load_group(1)
         w1_raw = stage.tile([P, PACK, F0], BF16, name="w1_raw")
         for u in range(2):
             nc.sync.dma_start(
@@ -158,7 +157,7 @@ def tile_intermodule_pa_t_kernel(tc, x, w1_l0, w1_l1, w2_l0, w2_l1, out):
                 out=x0_grouped[:].bitcast(F32).rearrange("p (t u) -> p t u", u=2),
                 in_=x0_t.rearrange("p u t -> p t u"),
             )
-            x1t = short.tile([P, D1, P], BF16, name="x1t")
+            x1t = waiting.tile([P, D1, P], BF16, name="x1t")
             nc.vector.tensor_copy(out=x1t[:], in_=x1_t)
             x0_grouped_tiles[i] = x0_grouped
             x1t_tiles[i] = x1t
@@ -171,32 +170,45 @@ def tile_intermodule_pa_t_kernel(tc, x, w1_l0, w1_l1, w2_l0, w2_l1, out):
             )
             x0_codes[i] = (words, scales)
 
-        def y1_component(i, c):
-            if c == 0:
-                ys_tiles[i] = waiting.tile([P, D1, BANK], F32, name="ys")
-            y1 = ring.tile([P, PACK, P], F32, name="y1", tag="ring")
+        def y1_bank(pool, i, c):
+            y1 = pool.tile([P, PACK, P], F32, name="y1", tag="ring")
             for j in range(PACK):
                 nc.tensor.matmul(
                     y1[:, j, :], lhsT=w1l1[:, j, :], rhs=x1t_tiles[i][:, c, :],
                     start=True, stop=True,
                 )
+            return y1[:].rearrange("p j t -> p t j")
+
+        def square_last_component(i):
+            norm = waiting.tile([P, BANK], F32, name="norm")
+            nc.scalar.activation(
+                out=norm[:].rearrange("p (t j) -> p t j", j=PACK),
+                in_=y1_bank(ps_sq, i, D1 - 1),
+                func=ACT.Square,
+                scale=SCALE_Y1,
+            )
+            norm_tiles[i] = norm
+
+        def keep_component(i, c):
+            if c == 0:
+                ys_tiles[i] = waiting.tile([P, KEPT, BANK], F32, name="ys")
             nc.vector.tensor_scalar_mul(
                 out=ys_tiles[i][:, c, :].rearrange("p (t j) -> p t j", j=PACK),
-                in0=y1[:].rearrange("p j t -> p t j"),
+                in0=y1_bank(ring, i, c),
                 scalar1=SCALE_Y1,
             )
 
-        def square_y1(i):
-            sq = short.tile([P, D1, BANK], F32, name="sq")
+        def square_kept(i):
+            sq = short.tile([P, KEPT, BANK], F32, name="sq")
             nc.scalar.activation(out=sq[:], in_=ys_tiles[i][:], func=ACT.Square)
             sq_tiles[i] = sq
 
         def add_squares(i):
-            sq = sq_tiles[i]
-            norm = waiting.tile([P, BANK], F32, name="norm")
-            nc.gpsimd.tensor_tensor(out=norm[:], in0=sq[:, 0, :], in1=sq[:, 1, :], op=ALU.add)
-            nc.gpsimd.tensor_tensor(out=norm[:], in0=norm[:], in1=sq[:, 2, :], op=ALU.add)
-            norm_tiles[i] = norm
+            norm = norm_tiles[i]
+            for c in range(KEPT):
+                nc.gpsimd.tensor_tensor(
+                    out=norm[:], in0=norm[:], in1=sq_tiles[i][:, c, :], op=ALU.add
+                )
 
         def batch_roots(b):
             for i in range(BATCH * b, BATCH * (b + 1)):
@@ -207,39 +219,45 @@ def tile_intermodule_pa_t_kernel(tc, x, w1_l0, w1_l1, w2_l0, w2_l1, out):
             norm = norm_tiles[i]
             nc.scalar.activation(out=norm[:], in_=norm[:], func=ACT.Sigmoid)
 
-        def gate_y1(i):
-            h1 = short.tile([P, D1, BANK], BF16, name="h1", align_bytes=64)
+        def gate_kept(i):
+            h = short.tile([P, H_PLANES, BANK], BF16, name="h", align_bytes=64)
             nc.gpsimd.tensor_tensor(
-                out=h1[:, 0:GPSIMD_PARTS, :],
-                in0=ys_tiles[i][:, 0:GPSIMD_PARTS, :],
-                in1=norm_tiles[i][:].unsqueeze(1).to_broadcast([P, GPSIMD_PARTS, BANK]),
+                out=h[:, PASSES0 : PASSES0 + KEPT, :],
+                in0=ys_tiles[i][:],
+                in1=norm_tiles[i][:].unsqueeze(1).to_broadcast([P, KEPT, BANK]),
                 op=ALU.mult,
             )
-            for c in range(GPSIMD_PARTS, D1):
-                nc.vector.tensor_tensor(
-                    out=h1[:, c, :], in0=ys_tiles[i][:, c, :], in1=norm_tiles[i][:], op=ALU.mult
-                )
-            h1_tiles[i] = h1
+            h_tiles[i] = h
 
-        def quantise_h1(i):
-            words = short.tile([P, D1, P], U32, name="h1_words", align_bytes=64)
-            scales = short.tile([P, D1, P], U8, name="h1_scales", align_bytes=64)
-            for c in range(D1):
+        def gate_last_component(i):
+            nc.vector.scalar_tensor_tensor(
+                out=h_tiles[i][:, H_PLANES - 1, :].rearrange("p (t j) -> p t j", j=PACK),
+                in0=y1_bank(ring, i, D1 - 1),
+                scalar=SCALE_Y1,
+                in1=norm_tiles[i][:].rearrange("p (t j) -> p t j", j=PACK),
+                op0=ALU.mult,
+                op1=ALU.mult,
+            )
+
+        def quantise_h(i):
+            words = short.tile([P, H_PLANES, P], U32, name="h_words", align_bytes=64)
+            scales = short.tile([P, H_PLANES, P], U8, name="h_scales", align_bytes=64)
+            for planes in (slice(0, H_PLANES - 1), slice(H_PLANES - 1, H_PLANES)):
                 nc.vector.quantize_mx(
-                    out=words[:, c, :].bitcast(FP8X4),
-                    scales=scales[:, c, :],
-                    in_=h1_tiles[i][:, c, :],
+                    out=words[:, planes, :].rearrange("p n t -> p (n t)").bitcast(FP8X4),
+                    scales=scales[:, planes, :].rearrange("p n t -> p (n t)"),
+                    in_=h_tiles[i][:, planes, :].rearrange("p n c -> p (n c)"),
                 )
-            h1_codes[i] = (words, scales)
+            h_codes[i] = (words, scales)
 
         def second_vector_matmul(i):
-            words, scales = h1_codes[i]
+            words, scales = h_codes[i]
             o1_ps = ring.tile([P, D1, U1], F32, name="o1_ps", tag="ring")
             for c in range(D1):
                 nc.tensor.matmul_mx(
                     out=o1_ps[:, c, :],
-                    lhsT=words[:, c, :].bitcast(FP8X4),
-                    lhsT_scale=scales[:, c, :],
+                    lhsT=words[:, PASSES0 + c, :].bitcast(FP8X4),
+                    lhsT_scale=scales[:, PASSES0 + c, :],
                     rhs=w3_words[:].bitcast(FP8X4),
                     rhs_scale=w3_scales[:],
                     start=True,
@@ -282,30 +300,18 @@ def tile_intermodule_pa_t_kernel(tc, x, w1_l0, w1_l1, w2_l0, w2_l1, out):
             sig0_tiles[i] = sig0
 
         def gate_y0(i):
-            h0 = short.tile([P, PASSES0, BANK], BF16, name="h0", align_bytes=64)
             for g in range(PASSES0):
                 nc.vector.scalar_tensor_tensor(
-                    out=h0[:, g, :].rearrange("p (t j) -> p t j", j=PACK),
+                    out=h_tiles[i][:, g, :].rearrange("p (t j) -> p t j", j=PACK),
                     in0=y0_tiles[i][g][:].rearrange("p j t -> p t j"),
                     scalar=SCALE_Y0,
                     in1=sig0_tiles[i][:, g, :].rearrange("p (t j) -> p t j", j=PACK),
                     op0=ALU.mult,
                     op1=ALU.mult,
                 )
-            h0_tiles[i] = h0
-
-        def quantise_h0(i):
-            words = short.tile([P, PASSES0, P], U32, name="h0_words", align_bytes=64)
-            scales = short.tile([P, PASSES0, P], U8, name="h0_scales", align_bytes=64)
-            nc.vector.quantize_mx(
-                out=words[:].rearrange("p g t -> p (g t)").bitcast(FP8X4),
-                scales=scales[:].rearrange("p g t -> p (g t)"),
-                in_=h0_tiles[i][:].rearrange("p g c -> p (g c)"),
-            )
-            h0_codes[i] = (words, scales)
 
         def second_scalar_matmul(i):
-            words, scales = h0_codes[i]
+            words, scales = h_codes[i]
             o0_ps = ring.tile([P, U0], F32, name="o0_ps", tag="ring")
             for g in range(PASSES0):
                 nc.tensor.matmul_mx(
@@ -329,24 +335,35 @@ def tile_intermodule_pa_t_kernel(tc, x, w1_l0, w1_l1, w2_l0, w2_l1, out):
             return 0 <= i < TILES
 
         pools.enter_context(tc.manual_schedule())
-        for step in range(-1, TILES + LAG + 3):
+        for step in range(-1, TILES + LAG + 2):
             front = step
             back = step - LAG
-            if step % GROUP == 0 and step // GROUP + 2 < TILES // GROUP:
-                load_group(step // GROUP + 2)
+            if (step + 1) % GROUP == 0 and (step + 1) // GROUP + 1 < TILES // GROUP:
+                load_group((step + 1) // GROUP + 1)
+            if is_tile(back):
+                gate_y0(back)
+            if is_tile(back + 1):
+                sigmoid_abs_y0(back + 1)
+            if is_tile(back - 1):
+                second_scalar_matmul(back - 1)
+                second_vector_matmul(back - 1)
+                store(back - 1)
+            if is_tile(front):
+                square_last_component(front)
             if is_tile(front + 1):
                 transpose_x(front + 1)
             if is_tile(front):
-                y1_component(front, 0)
+                keep_component(front, 0)
             if is_tile(front + 1):
                 quantise_x0(front + 1)
             if is_tile(front):
-                y1_component(front, 1)
-                y1_component(front, 2)
+                keep_component(front, 1)
             if is_tile(back):
-                sigmoid_abs_y0(back)
+                gate_last_component(back)
+            if is_tile(back + 2):
+                first_scalar_matmul(back + 2)
             if is_tile(front - 1):
-                square_y1(front - 1)
+                square_kept(front - 1)
             if 0 <= step < PASSES0:
                 regroup_w1(step)
             if PASSES0 <= step < 2 * PASSES0:
@@ -355,21 +372,11 @@ def tile_intermodule_pa_t_kernel(tc, x, w1_l0, w1_l1, w2_l0, w2_l1, out):
                 quantise_weights()
             if is_tile(front - 2):
                 add_squares(front - 2)
-            if is_tile(back + 1) and (back + 1) % BATCH == 0:
-                batch_roots((back + 1) // BATCH)
+            if is_tile(back + 2) and (back + 2) % BATCH == 0:
+                batch_roots((back + 2) // BATCH)
+            if is_tile(back + 2):
+                sigmoid_norm(back + 2)
             if is_tile(back + 1):
-                sigmoid_norm(back + 1)
+                gate_kept(back + 1)
             if is_tile(back):
-                gate_y1(back)
-                gate_y0(back)
-            if is_tile(back - 1):
-                second_scalar_matmul(back - 1)
-            if is_tile(back):
-                quantise_h0(back)
-            if is_tile(back - 1):
-                quantise_h1(back - 1)
-            if is_tile(back - 2):
-                second_vector_matmul(back - 2)
-                store(back - 2)
-            if is_tile(back + 1):
-                first_scalar_matmul(back + 1)
+                quantise_h(back)

@@ -45,6 +45,8 @@ def tile_intermodule_pa_t_kernel(tc, x, w1_l0, w1_l1, w2_l0, w2_l1, out):
         short = pools.enter_context(tc.tile_pool(name="short", bufs=2))
         waiting = pools.enter_context(tc.tile_pool(name="waiting", bufs=LAG + 2))
         o_pool = pools.enter_context(tc.tile_pool(name="o_pool", bufs=4))
+        h_pool = pools.enter_context(tc.tile_pool(name="h_pool", bufs=1))
+        sq_pool = pools.enter_context(tc.tile_pool(name="sq_pool", bufs=3))
         ps_y0 = pools.enter_context(tc.psum_pool(name="ps_y0", bufs=2 * PASSES0))
         ring = pools.enter_context(tc.psum_pool(name="ring", bufs=3))
         ps_sq = pools.enter_context(tc.psum_pool(name="ps_sq", bufs=1))
@@ -199,16 +201,13 @@ def tile_intermodule_pa_t_kernel(tc, x, w1_l0, w1_l1, w2_l0, w2_l1, out):
             )
 
         def square_kept(i):
-            sq = short.tile([P, KEPT, BANK], F32, name="sq")
+            sq = sq_pool.tile([P, KEPT, BANK], F32, name="sq")
             nc.scalar.activation(out=sq[:], in_=ys_tiles[i][:], func=ACT.Square)
             sq_tiles[i] = sq
 
-        def add_squares(i):
+        def add_square(i, c):
             norm = norm_tiles[i]
-            for c in range(KEPT):
-                nc.gpsimd.tensor_tensor(
-                    out=norm[:], in0=norm[:], in1=sq_tiles[i][:, c, :], op=ALU.add
-                )
+            nc.gpsimd.tensor_tensor(out=norm[:], in0=norm[:], in1=sq_tiles[i][:, c, :], op=ALU.add)
 
         def batch_roots(b):
             for i in range(BATCH * b, BATCH * (b + 1)):
@@ -219,15 +218,15 @@ def tile_intermodule_pa_t_kernel(tc, x, w1_l0, w1_l1, w2_l0, w2_l1, out):
             norm = norm_tiles[i]
             nc.scalar.activation(out=norm[:], in_=norm[:], func=ACT.Sigmoid)
 
-        def gate_kept(i):
-            h = short.tile([P, H_PLANES, BANK], BF16, name="h", align_bytes=64)
+        def gate_kept(i, c):
+            if c == 0:
+                h_tiles[i] = h_pool.tile([P, H_PLANES, BANK], BF16, name="h", align_bytes=64)
             nc.gpsimd.tensor_tensor(
-                out=h[:, PASSES0 : PASSES0 + KEPT, :],
-                in0=ys_tiles[i][:],
-                in1=norm_tiles[i][:].unsqueeze(1).to_broadcast([P, KEPT, BANK]),
+                out=h_tiles[i][:, PASSES0 + c, :],
+                in0=ys_tiles[i][:, c, :],
+                in1=norm_tiles[i][:],
                 op=ALU.mult,
             )
-            h_tiles[i] = h
 
         def gate_last_component(i):
             nc.vector.scalar_tensor_tensor(
@@ -354,9 +353,6 @@ def tile_intermodule_pa_t_kernel(tc, x, w1_l0, w1_l1, w2_l0, w2_l1, out):
                 transpose_x(front + 1)
             if is_tile(front):
                 keep_component(front, 0)
-            if is_tile(front + 1):
-                quantise_x0(front + 1)
-            if is_tile(front):
                 keep_component(front, 1)
             if is_tile(back):
                 gate_last_component(back)
@@ -370,13 +366,16 @@ def tile_intermodule_pa_t_kernel(tc, x, w1_l0, w1_l1, w2_l0, w2_l1, out):
                 regroup_w2(step - PASSES0)
             if step == 2 * PASSES0:
                 quantise_weights()
-            if is_tile(front - 2):
-                add_squares(front - 2)
             if is_tile(back + 2) and (back + 2) % BATCH == 0:
                 batch_roots((back + 2) // BATCH)
             if is_tile(back + 2):
                 sigmoid_norm(back + 2)
-            if is_tile(back + 1):
-                gate_kept(back + 1)
             if is_tile(back):
                 quantise_h(back)
+            if is_tile(front + 1):
+                quantise_x0(front + 1)
+            for c in range(KEPT):
+                if is_tile(front - 2):
+                    add_square(front - 2, c)
+                if is_tile(back + 1):
+                    gate_kept(back + 1, c)

@@ -207,7 +207,8 @@ def tile_intermodule_pa_t_kernel(tc, x, w1_l0, w1_l1, w2_l0, w2_l1, out):
 
         def add_square(i, c):
             norm = norm_tiles[i]
-            nc.gpsimd.tensor_tensor(out=norm[:], in0=norm[:], in1=sq_tiles[i][:, c, :], op=ALU.add)
+            engine = nc.gpsimd if c == 0 else nc.vector
+            engine.tensor_tensor(out=norm[:], in0=norm[:], in1=sq_tiles[i][:, c, :], op=ALU.add)
 
         def batch_roots(b):
             for i in range(BATCH * b, BATCH * (b + 1)):

@@ -66,7 +66,11 @@ def tile_intermodule_pa_t_kernel(tc, x, w1_l0, w1_l1, w2_l0, w2_l1, out):
 
         def load_group(g):
             xg = x_pool.tile([P, GROUP, X_COLS], BF16, name="xg")
-            nc.sync.dma_start(out=xg[:], in_=x_groups[g])
+            if g == 0:
+                for a in range(GROUP):
+                    nc.sync.dma_start(out=xg[:, a, :], in_=x_groups[g][:, a, :])
+            else:
+                nc.sync.dma_start(out=xg[:], in_=x_groups[g])
             x_tiles[g] = xg
 
         load_group(0)
@@ -114,15 +118,19 @@ def tile_intermodule_pa_t_kernel(tc, x, w1_l0, w1_l1, w2_l0, w2_l1, out):
             )
 
         def regroup_w2(g):
-            nc.scalar.copy(out=w2_grouped[:, g], in_=w2_raw[:, g].rearrange("p j n -> p n j"))
+            nc.vector.tensor_copy(
+                out=w2_grouped[:, g], in_=w2_raw[:, g].rearrange("p j n -> p n j")
+            )
 
-        def quantise_weights():
-            nc.vector.tensor_copy(out=w3_grouped[:], in_=w3_raw[:].rearrange("p j w -> p w j"))
+        def quantise_w1():
             nc.vector.quantize_mx(
                 out=w1_words[:].bitcast(FP8X4),
                 scales=w1_scales[:],
                 in_=w1_grouped[:].rearrange("p f t -> p (f t)"),
             )
+
+        def quantise_w2_w3():
+            nc.vector.tensor_copy(out=w3_grouped[:], in_=w3_raw[:].rearrange("p j w -> p w j"))
             nc.vector.quantize_mx(
                 out=w2_words[:].bitcast(FP8X4),
                 scales=w2_scales[:],
@@ -361,12 +369,14 @@ def tile_intermodule_pa_t_kernel(tc, x, w1_l0, w1_l1, w2_l0, w2_l1, out):
                 first_scalar_matmul(back + 2)
             if is_tile(front - 1):
                 square_kept(front - 1)
-            if 0 <= step < PASSES0:
-                regroup_w1(step)
-            if PASSES0 <= step < 2 * PASSES0:
-                regroup_w2(step - PASSES0)
-            if step == 2 * PASSES0:
-                quantise_weights()
+            if 2 <= step < 2 + PASSES0:
+                regroup_w1(step - 2)
+            if step == 2 + 2 * PASSES0:
+                quantise_w1()
+            if step == LAG - 1:
+                for g in range(PASSES0):
+                    regroup_w2(g)
+                quantise_w2_w3()
             if is_tile(back + 2) and (back + 2) % BATCH == 0:
                 batch_roots((back + 2) // BATCH)
             if is_tile(back + 2):

@@ -73,9 +73,9 @@ def tile_intermodule_pa_t_kernel(tc, x, w1_l0, w1_l1, w2_l0, w2_l1, out):
                 nc.sync.dma_start(out=xg[:], in_=x_groups[g])
             x_tiles[g] = xg
 
-        load_group(0)
         w1l1_raw = stage.tile([P, F1], BF16, name="w1l1_raw")
         nc.sync.dma_start(out=w1l1_raw[:], in_=w1_l1)
+        load_group(0)
         w1_raw = stage.tile([P, PACK, F0], BF16, name="w1_raw")
         for u in range(2):
             nc.sync.dma_start(
@@ -107,14 +107,18 @@ def tile_intermodule_pa_t_kernel(tc, x, w1_l0, w1_l1, w2_l0, w2_l1, out):
         w3_words = const.tile([P, U1], U32, name="w3_words", align_bytes=64)
         w3_scales = const.tile([P, U1], U8, name="w3_scales", align_bytes=64)
 
-        def regroup_w1(g):
+        def regroup_w1(piece):
+            g, js = piece // 2, slice(piece % 2 * 2, piece % 2 * 2 + 2)
+            return regroup_w1_(g, js)
+
+        def regroup_w1_(g, js):
             nc.scalar.copy(
                 out=w1_grouped[:, BANK * g : BANK * (g + 1), :].rearrange(
                     "p (j q) t -> p j q t", j=PACK
-                ),
+                )[:, js],
                 in_=w1_raw[:, :, BANK * g : BANK * (g + 1)].rearrange(
                     "p t (q j) -> p j q t", j=PACK
-                ),
+                )[:, js],
             )
 
         def regroup_w2(g):
@@ -129,17 +133,19 @@ def tile_intermodule_pa_t_kernel(tc, x, w1_l0, w1_l1, w2_l0, w2_l1, out):
                 in_=w1_grouped[:].rearrange("p f t -> p (f t)"),
             )
 
-        def quantise_w2_w3():
+        def prepare_w2_w3():
             nc.vector.tensor_copy(out=w3_grouped[:], in_=w3_raw[:].rearrange("p j w -> p w j"))
-            nc.vector.quantize_mx(
-                out=w2_words[:].bitcast(FP8X4),
-                scales=w2_scales[:],
-                in_=w2_grouped[:].rearrange("p g n j -> p (g n j)"),
-            )
+            for g in range(PASSES0):
+                regroup_w2(g)
             nc.vector.quantize_mx(
                 out=w3_words[:].bitcast(FP8X4),
                 scales=w3_scales[:],
                 in_=w3_grouped[:].rearrange("p w j -> p (w j)"),
+            )
+            nc.vector.quantize_mx(
+                out=w2_words[:].bitcast(FP8X4),
+                scales=w2_scales[:],
+                in_=w2_grouped[:].rearrange("p g n j -> p (g n j)"),
             )
 
         def transpose_x(i):
@@ -227,13 +233,14 @@ def tile_intermodule_pa_t_kernel(tc, x, w1_l0, w1_l1, w2_l0, w2_l1, out):
             norm = norm_tiles[i]
             nc.scalar.activation(out=norm[:], in_=norm[:], func=ACT.Sigmoid)
 
-        def gate_kept(i, c):
+        def gate_kept(i, c, engine, n=1):
             if c == 0:
                 h_tiles[i] = h_pool.tile([P, H_PLANES, BANK], BF16, name="h", align_bytes=64)
-            nc.gpsimd.tensor_tensor(
-                out=h_tiles[i][:, PASSES0 + c, :],
-                in0=ys_tiles[i][:, c, :],
-                in1=norm_tiles[i][:],
+            cs = slice(c, c + n)
+            engine.tensor_tensor(
+                out=h_tiles[i][:, PASSES0 + c : PASSES0 + c + n, :],
+                in0=ys_tiles[i][:, cs, :],
+                in1=norm_tiles[i][:].unsqueeze(1).to_broadcast([P, n, BANK]),
                 op=ALU.mult,
             )
 
@@ -318,7 +325,7 @@ def tile_intermodule_pa_t_kernel(tc, x, w1_l0, w1_l1, w2_l0, w2_l1, out):
                     op1=ALU.mult,
                 )
 
-        def second_scalar_matmul(i):
+        def second_scalar_matmul(i, on_scalar):
             words, scales = h_codes[i]
             o0_ps = ring.tile([P, U0], F32, name="o0_ps", tag="ring")
             for g in range(PASSES0):
@@ -332,9 +339,11 @@ def tile_intermodule_pa_t_kernel(tc, x, w1_l0, w1_l1, w2_l0, w2_l1, out):
                     stop=(g == PASSES0 - 1),
                 )
             out_tiles[i] = o_pool.tile([P, X_COLS], F32, name="out_tile")
-            nc.vector.tensor_scalar_mul(
-                out=out_tiles[i][:, 0:U0], in0=o0_ps[:], scalar1=SCALE_O0
-            )
+            o0 = out_tiles[i][:, 0:U0]
+            if on_scalar:
+                nc.scalar.mul(o0, o0_ps[:], SCALE_O0)
+            else:
+                nc.vector.tensor_scalar_mul(out=o0, in0=o0_ps[:], scalar1=SCALE_O0)
 
         def store(i):
             nc.sync.dma_start(out=out_groups[i // GROUP][:, i % GROUP, :], in_=out_tiles[i][:])
@@ -345,6 +354,8 @@ def tile_intermodule_pa_t_kernel(tc, x, w1_l0, w1_l1, w2_l0, w2_l1, out):
         pools.enter_context(tc.manual_schedule())
         for step in range(-1, TILES + LAG + 2):
             front = step
+            drain = front >= TILES
+            o0_scalar = front > TILES + 3
             back = step - LAG
             if (step + 1) % GROUP == 0 and (step + 1) // GROUP + 1 < TILES // GROUP:
                 load_group((step + 1) // GROUP + 1)
@@ -352,8 +363,10 @@ def tile_intermodule_pa_t_kernel(tc, x, w1_l0, w1_l1, w2_l0, w2_l1, out):
                 gate_y0(back)
             if is_tile(back + 1):
                 sigmoid_abs_y0(back + 1)
+                if (back + 1) % BATCH == 0:
+                    sigmoid_norm(back + 1)
             if is_tile(back - 1):
-                second_scalar_matmul(back - 1)
+                second_scalar_matmul(back - 1, o0_scalar)
                 second_vector_matmul(back - 1)
                 store(back - 1)
             if is_tile(front):
@@ -364,29 +377,29 @@ def tile_intermodule_pa_t_kernel(tc, x, w1_l0, w1_l1, w2_l0, w2_l1, out):
                 keep_component(front, 0)
                 keep_component(front, 1)
             if is_tile(back):
+                if drain:
+                    gate_kept(back, 1, nc.vector)
                 gate_last_component(back)
             if is_tile(back + 2):
                 first_scalar_matmul(back + 2)
             if is_tile(front - 1):
                 square_kept(front - 1)
-            if 2 <= step < 2 + PASSES0:
-                regroup_w1(step - 2)
-            if step == 2 + 2 * PASSES0:
+            if 4 <= step < 4 + 4:
+                regroup_w1(step - 4)
+            if step == 9:
                 quantise_w1()
-            if step == LAG - 1:
-                for g in range(PASSES0):
-                    regroup_w2(g)
-                quantise_w2_w3()
             if is_tile(back + 2) and (back + 2) % BATCH == 0:
                 batch_roots((back + 2) // BATCH)
-            if is_tile(back + 2):
+            if is_tile(back + 2) and (back + 2) % BATCH != 0:
                 sigmoid_norm(back + 2)
             if is_tile(back):
                 quantise_h(back)
             if is_tile(front + 1):
                 quantise_x0(front + 1)
-            for c in range(KEPT):
-                if is_tile(front - 2):
-                    add_square(front - 2, c)
-                if is_tile(back + 1):
-                    gate_kept(back + 1, c)
+            if is_tile(front - 2):
+                add_square(front - 2, 0)
+                add_square(front - 2, 1)
+            if is_tile(back + 1):
+                gate_kept(back + 1, 0, nc.gpsimd, 1 if front + 1 >= TILES else 2)
+            if step == LAG - 1:
+                prepare_w2_w3()

@@ -45,6 +45,7 @@ def tile_intermodule_pa_t_kernel(tc, x, w1_l0, w1_l1, w2_l0, w2_l1, out):
         short = pools.enter_context(tc.tile_pool(name="short", bufs=2))
         waiting = pools.enter_context(tc.tile_pool(name="waiting", bufs=LAG + 2))
         o_pool = pools.enter_context(tc.tile_pool(name="o_pool", bufs=4))
+        h0_pool = pools.enter_context(tc.tile_pool(name="h0_pool", bufs=2))
         h_pool = pools.enter_context(tc.tile_pool(name="h_pool", bufs=1))
         sq_pool = pools.enter_context(tc.tile_pool(name="sq_pool", bufs=3))
         ps_y0 = pools.enter_context(tc.psum_pool(name="ps_y0", bufs=2 * PASSES0))
@@ -60,6 +61,7 @@ def tile_intermodule_pa_t_kernel(tc, x, w1_l0, w1_l1, w2_l0, w2_l1, out):
         norm_tiles = {}
         y0_tiles = {}
         sig0_tiles = {}
+        h0_tiles = {}
         h_tiles = {}
         h_codes = {}
         out_tiles = {}
@@ -112,13 +114,17 @@ def tile_intermodule_pa_t_kernel(tc, x, w1_l0, w1_l1, w2_l0, w2_l1, out):
             return regroup_w1_(g, js)
 
         def regroup_w1_(g, js):
-            nc.scalar.copy(
+            nc.gpsimd.tensor_scalar(
                 out=w1_grouped[:, BANK * g : BANK * (g + 1), :].rearrange(
                     "p (j q) t -> p j q t", j=PACK
                 )[:, js],
-                in_=w1_raw[:, :, BANK * g : BANK * (g + 1)].rearrange(
+                in0=w1_raw[:, :, BANK * g : BANK * (g + 1)].rearrange(
                     "p t (q j) -> p j q t", j=PACK
                 )[:, js],
+                scalar1=1.0,
+                scalar2=0.0,
+                op0=ALU.mult,
+                op1=ALU.add,
             )
 
         def regroup_w2(g):
@@ -235,10 +241,10 @@ def tile_intermodule_pa_t_kernel(tc, x, w1_l0, w1_l1, w2_l0, w2_l1, out):
 
         def gate_kept(i, c, engine, n=1):
             if c == 0:
-                h_tiles[i] = h_pool.tile([P, H_PLANES, BANK], BF16, name="h", align_bytes=64)
+                h_tiles[i] = h_pool.tile([P, D1, BANK], BF16, name="h", align_bytes=64)
             cs = slice(c, c + n)
             engine.tensor_tensor(
-                out=h_tiles[i][:, PASSES0 + c : PASSES0 + c + n, :],
+                out=h_tiles[i][:, c : c + n, :],
                 in0=ys_tiles[i][:, cs, :],
                 in1=norm_tiles[i][:].unsqueeze(1).to_broadcast([P, n, BANK]),
                 op=ALU.mult,
@@ -246,7 +252,7 @@ def tile_intermodule_pa_t_kernel(tc, x, w1_l0, w1_l1, w2_l0, w2_l1, out):
 
         def gate_last_component(i):
             nc.vector.scalar_tensor_tensor(
-                out=h_tiles[i][:, H_PLANES - 1, :].rearrange("p (t j) -> p t j", j=PACK),
+                out=h_tiles[i][:, D1 - 1, :].rearrange("p (t j) -> p t j", j=PACK),
                 in0=y1_bank(ring, i, D1 - 1),
                 scalar=SCALE_Y1,
                 in1=norm_tiles[i][:].rearrange("p (t j) -> p t j", j=PACK),
@@ -257,11 +263,11 @@ def tile_intermodule_pa_t_kernel(tc, x, w1_l0, w1_l1, w2_l0, w2_l1, out):
         def quantise_h(i):
             words = short.tile([P, H_PLANES, P], U32, name="h_words", align_bytes=64)
             scales = short.tile([P, H_PLANES, P], U8, name="h_scales", align_bytes=64)
-            for planes in (slice(0, H_PLANES - 1), slice(H_PLANES - 1, H_PLANES)):
+            for tiles, first, start, n in ((h0_tiles, 0, 0, PASSES0), (h_tiles, PASSES0, 0, KEPT), (h_tiles, PASSES0 + KEPT, KEPT, 1)):
                 nc.vector.quantize_mx(
-                    out=words[:, planes, :].rearrange("p n t -> p (n t)").bitcast(FP8X4),
-                    scales=scales[:, planes, :].rearrange("p n t -> p (n t)"),
-                    in_=h_tiles[i][:, planes, :].rearrange("p n c -> p (n c)"),
+                    out=words[:, first : first + n, :].rearrange("p n t -> p (n t)").bitcast(FP8X4),
+                    scales=scales[:, first : first + n, :].rearrange("p n t -> p (n t)"),
+                    in_=tiles[i][:, start : start + n, :].rearrange("p n c -> p (n c)"),
                 )
             h_codes[i] = (words, scales)
 
@@ -311,13 +317,15 @@ def tile_intermodule_pa_t_kernel(tc, x, w1_l0, w1_l1, w2_l0, w2_l1, out):
                     func=ACT.Abs,
                     scale=SCALE_Y0,
                 )
-            nc.scalar.activation(out=sig0[:], in_=sig0[:], func=ACT.Sigmoid)
+            for g in range(PASSES0):
+                nc.scalar.activation(out=sig0[:, g, :], in_=sig0[:, g, :], func=ACT.Sigmoid)
             sig0_tiles[i] = sig0
 
         def gate_y0(i):
+            h0_tiles[i] = h0_pool.tile([P, PASSES0, BANK], BF16, name="h0", align_bytes=64)
             for g in range(PASSES0):
                 nc.vector.scalar_tensor_tensor(
-                    out=h_tiles[i][:, g, :].rearrange("p (t j) -> p t j", j=PACK),
+                    out=h0_tiles[i][:, g, :].rearrange("p (t j) -> p t j", j=PACK),
                     in0=y0_tiles[i][g][:].rearrange("p j t -> p t j"),
                     scalar=SCALE_Y0,
                     in1=sig0_tiles[i][:, g, :].rearrange("p (t j) -> p t j", j=PACK),
@@ -384,8 +392,9 @@ def tile_intermodule_pa_t_kernel(tc, x, w1_l0, w1_l1, w2_l0, w2_l1, out):
                 first_scalar_matmul(back + 2)
             if is_tile(front - 1):
                 square_kept(front - 1)
-            if 4 <= step < 4 + 4:
-                regroup_w1(step - 4)
+            if step == 0:
+                for piece in range(4):
+                    regroup_w1(piece)
             if step == 9:
                 quantise_w1()
             if is_tile(back + 2) and (back + 2) % BATCH == 0:
@@ -396,10 +405,10 @@ def tile_intermodule_pa_t_kernel(tc, x, w1_l0, w1_l1, w2_l0, w2_l1, out):
                 quantise_h(back)
             if is_tile(front + 1):
                 quantise_x0(front + 1)
-            if is_tile(front - 2):
-                add_square(front - 2, 0)
-                add_square(front - 2, 1)
-            if is_tile(back + 1):
-                gate_kept(back + 1, 0, nc.gpsimd, 1 if front + 1 >= TILES else 2)
             if step == LAG - 1:
                 prepare_w2_w3()
+            if is_tile(front - 2):
+                for c in (1, 0) if front < LAG else (0, 1):
+                    add_square(front - 2, c)
+            if is_tile(back + 1):
+                gate_kept(back + 1, 0, nc.gpsimd, 1 if front + 1 >= TILES else 2)

@@ -18,7 +18,9 @@ N_TOK, U0, U1, F0, F1, D1 = 4096, 512, 128, 1024, 512, 3
 X_COLS = U0 + U1 * D1
 TILES = N_TOK // P
 GROUP = 4
-BATCH = 8
+N_BATCHES = 6
+STARTS = [TILES * k // N_BATCHES for k in range(N_BATCHES + 1)]
+BATCH = max(b - a for a, b in zip(STARTS, STARTS[1:]))
 PASSES0 = F0 // (P * PACK)
 BANK = 512
 LAG = BATCH + 4
@@ -180,7 +182,10 @@ def tile_intermodule_pa_t_kernel(tc, x, w1_l0, w1_l1, w2_l0, w2_l1, out):
                 in_=x0_t.rearrange("p u t -> p t u"),
             )
             x1t = waiting.tile([P, D1, P], BF16, name="x1t")
-            nc.vector.tensor_copy(out=x1t[:], in_=x1_t)
+            if i < 8:
+                nc.scalar.copy(out=x1t[:], in_=x1_t)
+            else:
+                nc.vector.tensor_copy(out=x1t[:], in_=x1_t)
             x0_grouped_tiles[i] = x0_grouped
             x1t_tiles[i] = x1t
 
@@ -231,7 +236,7 @@ def tile_intermodule_pa_t_kernel(tc, x, w1_l0, w1_l1, w2_l0, w2_l1, out):
             engine.tensor_tensor(out=norm[:], in0=norm[:], in1=sq_tiles[i][:, c, :], op=ALU.add)
 
         def batch_roots(b):
-            for i in range(BATCH * b, BATCH * (b + 1)):
+            for i in range(STARTS[b], STARTS[b + 1]):
                 norm = norm_tiles[i]
                 nc.scalar.activation(out=norm[:], in_=norm[:], func=ACT.Sqrt)
 
@@ -362,7 +367,7 @@ def tile_intermodule_pa_t_kernel(tc, x, w1_l0, w1_l1, w2_l0, w2_l1, out):
         pools.enter_context(tc.manual_schedule())
         for step in range(-1, TILES + LAG + 2):
             front = step
-            drain = front >= TILES
+            drain = front >= TILES + 0
             o0_scalar = front > TILES + 3
             back = step - LAG
             if (step + 1) % GROUP == 0 and (step + 1) // GROUP + 1 < TILES // GROUP:
@@ -371,7 +376,7 @@ def tile_intermodule_pa_t_kernel(tc, x, w1_l0, w1_l1, w2_l0, w2_l1, out):
                 gate_y0(back)
             if is_tile(back + 1):
                 sigmoid_abs_y0(back + 1)
-                if (back + 1) % BATCH == 0:
+                if back + 1 in STARTS:
                     sigmoid_norm(back + 1)
             if is_tile(back - 1):
                 second_scalar_matmul(back - 1, o0_scalar)
@@ -395,11 +400,11 @@ def tile_intermodule_pa_t_kernel(tc, x, w1_l0, w1_l1, w2_l0, w2_l1, out):
             if step == 0:
                 for piece in range(4):
                     regroup_w1(piece)
-            if step == 9:
+            if step == min(9, LAG - 3):
                 quantise_w1()
-            if is_tile(back + 2) and (back + 2) % BATCH == 0:
-                batch_roots((back + 2) // BATCH)
-            if is_tile(back + 2) and (back + 2) % BATCH != 0:
+            if is_tile(back + 2) and back + 2 in STARTS:
+                batch_roots(STARTS.index(back + 2))
+            if is_tile(back + 2) and back + 2 not in STARTS:
                 sigmoid_norm(back + 2)
             if is_tile(back):
                 quantise_h(back)
@@ -408,7 +413,7 @@ def tile_intermodule_pa_t_kernel(tc, x, w1_l0, w1_l1, w2_l0, w2_l1, out):
             if step == LAG - 1:
                 prepare_w2_w3()
             if is_tile(front - 2):
-                for c in (1, 0) if front < LAG else (0, 1):
+                for c in (1, 0):
                     add_square(front - 2, c)
             if is_tile(back + 1):
-                gate_kept(back + 1, 0, nc.gpsimd, 1 if front + 1 >= TILES else 2)
+                gate_kept(back + 1, 0, nc.gpsimd, 1 if front + 1 >= TILES + 0 else 2)

@@ -55,6 +55,13 @@ def tile_intermodule_pa_t_kernel(tc, x, w1_l0, w1_l1, w2_l0, w2_l1, out):
         ps_sq = pools.enter_context(tc.psum_pool(name="ps_sq", bufs=1))
 
         x_tiles = {}
+        pairs = [None]
+        last_codes = {}
+
+        def new_pair():
+            if pairs[0] is None:
+                pairs[0] = short.tile([P, 2, BANK], BF16, name="pair", align_bytes=64)
+
         x1t_tiles = {}
         x0_grouped_tiles = {}
         x0_codes = {}
@@ -176,9 +183,10 @@ def tile_intermodule_pa_t_kernel(tc, x, w1_l0, w1_l1, w2_l0, w2_l1, out):
                 nc.tensor.transpose(
                     x1_t[:, c, :], xg[:, a, U0 + c : X_COLS : D1], ident_bf16[:]
                 )
-            x0_grouped = short.tile([P, P * PACK], BF16, name="x0_grouped", align_bytes=64)
+            new_pair()
+            x0_grouped = pairs[0][:, 1, :]
             nc.vector.tensor_copy(
-                out=x0_grouped[:].bitcast(F32).rearrange("p (t u) -> p t u", u=2),
+                out=x0_grouped.bitcast(F32).rearrange("p (t u) -> p t u", u=2),
                 in_=x0_t.rearrange("p u t -> p t u"),
             )
             x1t = waiting.tile([P, D1, P], BF16, name="x1t")
@@ -189,13 +197,21 @@ def tile_intermodule_pa_t_kernel(tc, x, w1_l0, w1_l1, w2_l0, w2_l1, out):
             x0_grouped_tiles[i] = x0_grouped
             x1t_tiles[i] = x1t
 
-        def quantise_x0(i):
-            words = waiting.tile([P, P], U32, name="x0_words", align_bytes=64)
-            scales = waiting.tile([P, P], U8, name="x0_scales", align_bytes=64)
+        def quantise_pair(b, f):
+            lo, hi = (0 if is_tile(b) else 1), (2 if is_tile(f) else 1)
+            if lo == hi:
+                return
+            words = waiting.tile([P, 2, P], U32, name="pair_words", align_bytes=64)
+            scales = waiting.tile([P, 2, P], U8, name="pair_scales", align_bytes=64)
             nc.vector.quantize_mx(
-                out=words[:].bitcast(FP8X4), scales=scales[:], in_=x0_grouped_tiles[i][:]
+                out=words[:, lo:hi, :].rearrange("p n t -> p (n t)").bitcast(FP8X4),
+                scales=scales[:, lo:hi, :].rearrange("p n t -> p (n t)"),
+                in_=pairs[0][:, lo:hi, :].rearrange("p n c -> p (n c)"),
             )
-            x0_codes[i] = (words, scales)
+            if hi == 2:
+                x0_codes[f] = (words[:, 1, :], scales[:, 1, :])
+            if lo == 0:
+                last_codes[b] = (words[:, 0, :], scales[:, 0, :])
 
         def y1_bank(pool, i, c):
             y1 = pool.tile([P, PACK, P], F32, name="y1", tag="ring")
@@ -246,7 +262,7 @@ def tile_intermodule_pa_t_kernel(tc, x, w1_l0, w1_l1, w2_l0, w2_l1, out):
 
         def gate_kept(i, c, engine, n=1):
             if c == 0:
-                h_tiles[i] = h_pool.tile([P, D1, BANK], BF16, name="h", align_bytes=64)
+                h_tiles[i] = h_pool.tile([P, KEPT, BANK], BF16, name="h", align_bytes=64)
             cs = slice(c, c + n)
             engine.tensor_tensor(
                 out=h_tiles[i][:, c : c + n, :],
@@ -256,8 +272,9 @@ def tile_intermodule_pa_t_kernel(tc, x, w1_l0, w1_l1, w2_l0, w2_l1, out):
             )
 
         def gate_last_component(i):
+            new_pair()
             nc.vector.scalar_tensor_tensor(
-                out=h_tiles[i][:, D1 - 1, :].rearrange("p (t j) -> p t j", j=PACK),
+                out=pairs[0][:, 0, :].rearrange("p (t j) -> p t j", j=PACK),
                 in0=y1_bank(ring, i, D1 - 1),
                 scalar=SCALE_Y1,
                 in1=norm_tiles[i][:].rearrange("p (t j) -> p t j", j=PACK),
@@ -268,7 +285,7 @@ def tile_intermodule_pa_t_kernel(tc, x, w1_l0, w1_l1, w2_l0, w2_l1, out):
         def quantise_h(i):
             words = short.tile([P, H_PLANES, P], U32, name="h_words", align_bytes=64)
             scales = short.tile([P, H_PLANES, P], U8, name="h_scales", align_bytes=64)
-            for tiles, first, start, n in ((h0_tiles, 0, 0, PASSES0), (h_tiles, PASSES0, 0, KEPT), (h_tiles, PASSES0 + KEPT, KEPT, 1)):
+            for tiles, first, start, n in ((h0_tiles, 0, 0, PASSES0), (h_tiles, PASSES0, 0, KEPT)):
                 nc.vector.quantize_mx(
                     out=words[:, first : first + n, :].rearrange("p n t -> p (n t)").bitcast(FP8X4),
                     scales=scales[:, first : first + n, :].rearrange("p n t -> p (n t)"),
@@ -280,10 +297,14 @@ def tile_intermodule_pa_t_kernel(tc, x, w1_l0, w1_l1, w2_l0, w2_l1, out):
             words, scales = h_codes[i]
             o1_ps = ring.tile([P, D1, U1], F32, name="o1_ps", tag="ring")
             for c in range(D1):
+                if c < KEPT:
+                    w, s = words[:, PASSES0 + c, :], scales[:, PASSES0 + c, :]
+                else:
+                    w, s = last_codes[i]
                 nc.tensor.matmul_mx(
                     out=o1_ps[:, c, :],
-                    lhsT=words[:, PASSES0 + c, :].bitcast(FP8X4),
-                    lhsT_scale=scales[:, PASSES0 + c, :],
+                    lhsT=w.bitcast(FP8X4),
+                    lhsT_scale=s,
                     rhs=w3_words[:].bitcast(FP8X4),
                     rhs_scale=w3_scales[:],
                     start=True,
@@ -306,8 +327,8 @@ def tile_intermodule_pa_t_kernel(tc, x, w1_l0, w1_l1, w2_l0, w2_l1, out):
                         out=y0[:, j, :],
                         lhsT=w1_words[:, chunk].bitcast(FP8X4),
                         lhsT_scale=w1_scales[:, chunk],
-                        rhs=x_words[:].bitcast(FP8X4),
-                        rhs_scale=x_scales[:],
+                        rhs=x_words.bitcast(FP8X4),
+                        rhs_scale=x_scales,
                         start=True,
                         stop=True,
                     )
@@ -368,8 +389,8 @@ def tile_intermodule_pa_t_kernel(tc, x, w1_l0, w1_l1, w2_l0, w2_l1, out):
         for step in range(-1, TILES + LAG + 2):
             front = step
             drain = front >= TILES + 0
-            o0_scalar = front > TILES + 3
             back = step - LAG
+            o0_scalar = front > TILES + 3
             if (step + 1) % GROUP == 0 and (step + 1) // GROUP + 1 < TILES // GROUP:
                 load_group((step + 1) // GROUP + 1)
             if is_tile(back):
@@ -390,9 +411,9 @@ def tile_intermodule_pa_t_kernel(tc, x, w1_l0, w1_l1, w2_l0, w2_l1, out):
                 keep_component(front, 0)
                 keep_component(front, 1)
             if is_tile(back):
+                gate_last_component(back)
                 if drain:
                     gate_kept(back, 1, nc.vector)
-                gate_last_component(back)
             if is_tile(back + 2):
                 first_scalar_matmul(back + 2)
             if is_tile(front - 1):
@@ -408,8 +429,8 @@ def tile_intermodule_pa_t_kernel(tc, x, w1_l0, w1_l1, w2_l0, w2_l1, out):
                 sigmoid_norm(back + 2)
             if is_tile(back):
                 quantise_h(back)
-            if is_tile(front + 1):
-                quantise_x0(front + 1)
+            quantise_pair(back, front + 1)
+            pairs[0] = None
             if step == LAG - 1:
                 prepare_w2_w3()
             if is_tile(front - 2):

@@ -19,7 +19,8 @@ X_COLS = U0 + U1 * D1
 TILES = N_TOK // P
 GROUP = 4
 N_BATCHES = 6
-STARTS = [TILES * k // N_BATCHES for k in range(N_BATCHES + 1)]
+SIZES = [(TILES + k) // N_BATCHES for k in range(N_BATCHES)]
+STARTS = [sum(SIZES[:k]) for k in range(N_BATCHES + 1)]
 BATCH = max(b - a for a, b in zip(STARTS, STARTS[1:]))
 PASSES0 = F0 // (P * PACK)
 BANK = 512
@@ -343,9 +344,11 @@ def tile_intermodule_pa_t_kernel(tc, x, w1_l0, w1_l1, w2_l0, w2_l1, out):
                     func=ACT.Abs,
                     scale=SCALE_Y0,
                 )
-            for g in range(PASSES0):
-                nc.scalar.activation(out=sig0[:, g, :], in_=sig0[:, g, :], func=ACT.Sigmoid)
             sig0_tiles[i] = sig0
+
+        def sigmoid_y0(i, g):
+            sig0 = sig0_tiles[i]
+            nc.scalar.activation(out=sig0[:, g, :], in_=sig0[:, g, :], func=ACT.Sigmoid)
 
         def gate_y0(i):
             h0_tiles[i] = h0_pool.tile([P, PASSES0, BANK], BF16, name="h0", align_bytes=64)
@@ -397,10 +400,14 @@ def tile_intermodule_pa_t_kernel(tc, x, w1_l0, w1_l1, w2_l0, w2_l1, out):
                 gate_y0(back)
             if is_tile(back + 1):
                 sigmoid_abs_y0(back + 1)
+                sigmoid_y0(back + 1, 0)
                 if back + 1 in STARTS:
                     sigmoid_norm(back + 1)
             if is_tile(back - 1):
                 second_scalar_matmul(back - 1, o0_scalar)
+            if is_tile(back + 1):
+                sigmoid_y0(back + 1, 1)
+            if is_tile(back - 1):
                 second_vector_matmul(back - 1)
                 store(back - 1)
             if is_tile(front):

import math
from contextlib import ExitStack

import concourse.mybir as mybir
from concourse.masks import make_identity

F32 = mybir.dt.float32
BF16 = mybir.dt.bfloat16
U32 = mybir.dt.uint32
U8 = mybir.dt.uint8
FP8X4 = mybir.dt.float8_e4m3fn_x4
ACT = mybir.ActivationFunctionType
ALU = mybir.AluOpType

P = 128
PACK = 4
N_TOK, U0, U1, F0, F1, D1 = 4096, 512, 128, 1024, 512, 3
X_COLS = U0 + U1 * D1
TILES = N_TOK // P
GROUP = 4
N_BATCHES = 6
SIZES = [(TILES + k) // N_BATCHES for k in range(N_BATCHES)]
STARTS = [sum(SIZES[:k]) for k in range(N_BATCHES + 1)]
BATCH = max(b - a for a, b in zip(STARTS, STARTS[1:]))
PASSES0 = F0 // (P * PACK)
BANK = 512
LAG = BATCH + 4
KEPT = 2
H_PLANES = PASSES0 + D1

SCALE_Y0 = 1.0 / math.sqrt(U0)
SCALE_O0 = 1.0 / math.sqrt(F0)
SCALE_Y1 = 1.0 / math.sqrt(U1)
SCALE_O1 = 1.0 / math.sqrt(F1)

FLOPS = 2 * N_TOK * (U0 * F0 + F0 * U0 + D1 * U1 * F1 + D1 * F1 * U1)


def tile_intermodule_pa_t_kernel(tc, x, w1_l0, w1_l1, w2_l0, w2_l1, out):
    nc = tc.nc
    x_groups = x.rearrange("(g p a) c -> g p a c", p=P, a=GROUP)
    out_groups = out.rearrange("(g p a) c -> g p a c", p=P, a=GROUP)

    with ExitStack() as pools:
        const = pools.enter_context(tc.tile_pool(name="const", bufs=1))
        stage = pools.enter_context(tc.tile_pool(name="stage", bufs=1))
        x_pool = pools.enter_context(tc.tile_pool(name="x_pool", bufs=2))
        short = pools.enter_context(tc.tile_pool(name="short", bufs=2))
        waiting = pools.enter_context(tc.tile_pool(name="waiting", bufs=LAG + 2))
        o_pool = pools.enter_context(tc.tile_pool(name="o_pool", bufs=4))
        h0_pool = pools.enter_context(tc.tile_pool(name="h0_pool", bufs=2))
        h_pool = pools.enter_context(tc.tile_pool(name="h_pool", bufs=1))
        sq_pool = pools.enter_context(tc.tile_pool(name="sq_pool", bufs=3))
        ps_y0 = pools.enter_context(tc.psum_pool(name="ps_y0", bufs=2 * PASSES0))
        ring = pools.enter_context(tc.psum_pool(name="ring", bufs=3))
        ps_sq = pools.enter_context(tc.psum_pool(name="ps_sq", bufs=1))

        x_tiles = {}
        pairs = [None]
        last_codes = {}

        def new_pair():
            if pairs[0] is None:
                pairs[0] = short.tile([P, 2, BANK], BF16, name="pair", align_bytes=64)

        x1t_tiles = {}
        x0_grouped_tiles = {}
        x0_codes = {}
        ys_tiles = {}
        sq_tiles = {}
        norm_tiles = {}
        y0_tiles = {}
        sig0_tiles = {}
        h0_tiles = {}
        h_tiles = {}
        h_codes = {}
        out_tiles = {}

        def load_group(g):
            xg = x_pool.tile([P, GROUP, X_COLS], BF16, name="xg")
            if g == 0:
                for a in range(GROUP):
                    nc.sync.dma_start(out=xg[:, a, :], in_=x_groups[g][:, a, :])
            else:
                nc.sync.dma_start(out=xg[:], in_=x_groups[g])
            x_tiles[g] = xg

        w1l1_raw = stage.tile([P, F1], BF16, name="w1l1_raw")
        nc.sync.dma_start(out=w1l1_raw[:], in_=w1_l1)
        load_group(0)
        w1_raw = stage.tile([P, PACK, F0], BF16, name="w1_raw")
        for u in range(2):
            nc.sync.dma_start(
                out=w1_raw[:, 2 * u : 2 * u + 2, :],
                in_=w1_l0[256 * u : 256 * (u + 1), :].rearrange("(p e) f -> p e f", e=2),
            )
        w2_raw = stage.tile([P, PASSES0, PACK, U0], BF16, name="w2_raw")
        nc.sync.dma_start(
            out=w2_raw[:], in_=w2_l0.rearrange("(g p j) n -> p g j n", g=PASSES0, j=PACK)
        )
        w3_raw = stage.tile([P, PACK, U1], BF16, name="w3_raw")
        nc.sync.dma_start(out=w3_raw[:], in_=w2_l1.rearrange("(p j) w -> p j w", j=PACK))

        ident_f32 = const.tile([P, P], F32, name="ident_f32")
        make_identity(nc, ident_f32[:])
        ident_bf16 = const.tile([P, P], BF16, name="ident_bf16")
        make_identity(nc, ident_bf16[:])

        w1l1 = const.tile([P, PACK, P], BF16, name="w1l1")
        nc.vector.tensor_copy(out=w1l1[:], in_=w1l1_raw[:].rearrange("p (q j) -> p j q", j=PACK))

        w1_grouped = stage.tile([P, F0, PACK], BF16, name="w1_grouped", align_bytes=64)
        w2_grouped = stage.tile([P, PASSES0, U0, PACK], BF16, name="w2_grouped", align_bytes=64)
        w3_grouped = stage.tile([P, U1, PACK], BF16, name="w3_grouped", align_bytes=64)
        w1_words = const.tile([P, F0], U32, name="w1_words", align_bytes=64)
        w1_scales = const.tile([P, F0], U8, name="w1_scales", align_bytes=64)
        w2_words = const.tile([P, PASSES0 * U0], U32, name="w2_words", align_bytes=64)
        w2_scales = const.tile([P, PASSES0 * U0], U8, name="w2_scales", align_bytes=64)
        w3_words = const.tile([P, U1], U32, name="w3_words", align_bytes=64)
        w3_scales = const.tile([P, U1], U8, name="w3_scales", align_bytes=64)

        def regroup_w1(piece):
            g, js = piece // 2, slice(piece % 2 * 2, piece % 2 * 2 + 2)
            return regroup_w1_(g, js)

        def regroup_w1_(g, js):
            nc.gpsimd.tensor_scalar(
                out=w1_grouped[:, BANK * g : BANK * (g + 1), :].rearrange(
                    "p (j q) t -> p j q t", j=PACK
                )[:, js],
                in0=w1_raw[:, :, BANK * g : BANK * (g + 1)].rearrange(
                    "p t (q j) -> p j q t", j=PACK
                )[:, js],
                scalar1=1.0,
                scalar2=0.0,
                op0=ALU.mult,
                op1=ALU.add,
            )

        def regroup_w2(g):
            nc.vector.tensor_copy(
                out=w2_grouped[:, g], in_=w2_raw[:, g].rearrange("p j n -> p n j")
            )

        def quantise_w1():
            nc.vector.quantize_mx(
                out=w1_words[:].bitcast(FP8X4),
                scales=w1_scales[:],
                in_=w1_grouped[:].rearrange("p f t -> p (f t)"),
            )

        def prepare_w2_w3():
            nc.vector.tensor_copy(out=w3_grouped[:], in_=w3_raw[:].rearrange("p j w -> p w j"))
            for g in range(PASSES0):
                regroup_w2(g)
            nc.vector.quantize_mx(
                out=w3_words[:].bitcast(FP8X4),
                scales=w3_scales[:],
                in_=w3_grouped[:].rearrange("p w j -> p (w j)"),
            )
            nc.vector.quantize_mx(
                out=w2_words[:].bitcast(FP8X4),
                scales=w2_scales[:],
                in_=w2_grouped[:].rearrange("p g n j -> p (g n j)"),
            )

        def transpose_x(i):
            xg = x_tiles[i // GROUP]
            a = i % GROUP
            x_as_words = xg[:].rearrange("p a c -> p (a c)").bitcast(F32)
            first_word = a * (X_COLS // 2)
            xt = ring.tile([P, BANK], F32, name="xt", tag="ring")
            x0_t = xt[:, 0 : 2 * P].rearrange("p (u t) -> p u t", u=2)
            x1_t = xt[:, 2 * P : 2 * P + D1 * P // 2].bitcast(BF16).rearrange(
                "p (c t) -> p c t", c=D1
            )
            for u in range(2):
                nc.tensor.transpose(
                    x0_t[:, u, :],
                    x_as_words[:, first_word + P * u : first_word + P * (u + 1)],
                    ident_f32[:],
                )
            for c in range(D1):
                nc.tensor.transpose(
                    x1_t[:, c, :], xg[:, a, U0 + c : X_COLS : D1], ident_bf16[:]
                )
            new_pair()
            x0_grouped = pairs[0][:, 1, :]
            nc.vector.tensor_copy(
                out=x0_grouped.bitcast(F32).rearrange("p (t u) -> p t u", u=2),
                in_=x0_t.rearrange("p u t -> p t u"),
            )
            x1t = waiting.tile([P, D1, P], BF16, name="x1t")
            if i < 8:
                nc.scalar.copy(out=x1t[:], in_=x1_t)
            else:
                nc.vector.tensor_copy(out=x1t[:], in_=x1_t)
            x0_grouped_tiles[i] = x0_grouped
            x1t_tiles[i] = x1t

        def quantise_pair(b, f):
            lo, hi = (0 if is_tile(b) else 1), (2 if is_tile(f) else 1)
            if lo == hi:
                return
            words = waiting.tile([P, 2, P], U32, name="pair_words", align_bytes=64)
            scales = waiting.tile([P, 2, P], U8, name="pair_scales", align_bytes=64)
            nc.vector.quantize_mx(
                out=words[:, lo:hi, :].rearrange("p n t -> p (n t)").bitcast(FP8X4),
                scales=scales[:, lo:hi, :].rearrange("p n t -> p (n t)"),
                in_=pairs[0][:, lo:hi, :].rearrange("p n c -> p (n c)"),
            )
            if hi == 2:
                x0_codes[f] = (words[:, 1, :], scales[:, 1, :])
            if lo == 0:
                last_codes[b] = (words[:, 0, :], scales[:, 0, :])

        def y1_bank(pool, i, c):
            y1 = pool.tile([P, PACK, P], F32, name="y1", tag="ring")
            for j in range(PACK):
                nc.tensor.matmul(
                    y1[:, j, :], lhsT=w1l1[:, j, :], rhs=x1t_tiles[i][:, c, :],
                    start=True, stop=True,
                )
            return y1[:].rearrange("p j t -> p t j")

        def square_last_component(i):
            norm = waiting.tile([P, BANK], F32, name="norm")
            nc.scalar.activation(
                out=norm[:].rearrange("p (t j) -> p t j", j=PACK),
                in_=y1_bank(ps_sq, i, D1 - 1),
                func=ACT.Square,
                scale=SCALE_Y1,
            )
            norm_tiles[i] = norm

        def keep_component(i, c):
            if c == 0:
                ys_tiles[i] = waiting.tile([P, KEPT, BANK], F32, name="ys")
            nc.vector.tensor_scalar_mul(
                out=ys_tiles[i][:, c, :].rearrange("p (t j) -> p t j", j=PACK),
                in0=y1_bank(ring, i, c),
                scalar1=SCALE_Y1,
            )

        def square_kept(i):
            sq = sq_pool.tile([P, KEPT, BANK], F32, name="sq")
            nc.scalar.activation(out=sq[:], in_=ys_tiles[i][:], func=ACT.Square)
            sq_tiles[i] = sq

        def add_square(i, c):
            norm = norm_tiles[i]
            engine = nc.gpsimd if c == 0 else nc.vector
            engine.tensor_tensor(out=norm[:], in0=norm[:], in1=sq_tiles[i][:, c, :], op=ALU.add)

        def batch_roots(b):
            for i in range(STARTS[b], STARTS[b + 1]):
                norm = norm_tiles[i]
                nc.scalar.activation(out=norm[:], in_=norm[:], func=ACT.Sqrt)

        def sigmoid_norm(i):
            norm = norm_tiles[i]
            nc.scalar.activation(out=norm[:], in_=norm[:], func=ACT.Sigmoid)

        def gate_kept(i, c, engine, n=1):
            if c == 0:
                h_tiles[i] = h_pool.tile([P, KEPT, BANK], BF16, name="h", align_bytes=64)
            cs = slice(c, c + n)
            engine.tensor_tensor(
                out=h_tiles[i][:, c : c + n, :],
                in0=ys_tiles[i][:, cs, :],
                in1=norm_tiles[i][:].unsqueeze(1).to_broadcast([P, n, BANK]),
                op=ALU.mult,
            )

        def gate_last_component(i):
            new_pair()
            nc.vector.scalar_tensor_tensor(
                out=pairs[0][:, 0, :].rearrange("p (t j) -> p t j", j=PACK),
                in0=y1_bank(ring, i, D1 - 1),
                scalar=SCALE_Y1,
                in1=norm_tiles[i][:].rearrange("p (t j) -> p t j", j=PACK),
                op0=ALU.mult,
                op1=ALU.mult,
            )

        def quantise_h(i):
            words = short.tile([P, H_PLANES, P], U32, name="h_words", align_bytes=64)
            scales = short.tile([P, H_PLANES, P], U8, name="h_scales", align_bytes=64)
            for tiles, first, start, n in ((h0_tiles, 0, 0, PASSES0), (h_tiles, PASSES0, 0, KEPT)):
                nc.vector.quantize_mx(
                    out=words[:, first : first + n, :].rearrange("p n t -> p (n t)").bitcast(FP8X4),
                    scales=scales[:, first : first + n, :].rearrange("p n t -> p (n t)"),
                    in_=tiles[i][:, start : start + n, :].rearrange("p n c -> p (n c)"),
                )
            h_codes[i] = (words, scales)

        def second_vector_matmul(i):
            words, scales = h_codes[i]
            o1_ps = ring.tile([P, D1, U1], F32, name="o1_ps", tag="ring")
            for c in range(D1):
                if c < KEPT:
                    w, s = words[:, PASSES0 + c, :], scales[:, PASSES0 + c, :]
                else:
                    w, s = last_codes[i]
                nc.tensor.matmul_mx(
                    out=o1_ps[:, c, :],
                    lhsT=w.bitcast(FP8X4),
                    lhsT_scale=s,
                    rhs=w3_words[:].bitcast(FP8X4),
                    rhs_scale=w3_scales[:],
                    start=True,
                    stop=True,
                )
            nc.vector.tensor_scalar_mul(
                out=out_tiles[i][:, U0:X_COLS].rearrange("p (w c) -> p w c", c=D1),
                in0=o1_ps[:].rearrange("p c w -> p w c"),
                scalar1=SCALE_O1,
            )

        def first_scalar_matmul(i):
            x_words, x_scales = x0_codes[i]
            y0_tiles[i] = []
            for g in range(PASSES0):
                y0 = ps_y0.tile([P, PACK, P], F32, name="y0")
                for j in range(PACK):
                    chunk = slice(P * (PACK * g + j), P * (PACK * g + j + 1))
                    nc.tensor.matmul_mx(
                        out=y0[:, j, :],
                        lhsT=w1_words[:, chunk].bitcast(FP8X4),
                        lhsT_scale=w1_scales[:, chunk],
                        rhs=x_words.bitcast(FP8X4),
                        rhs_scale=x_scales,
                        start=True,
                        stop=True,
                    )
                y0_tiles[i].append(y0)

        def sigmoid_abs_y0(i):
            sig0 = short.tile([P, PASSES0, BANK], F32, name="sig0")
            for g in range(PASSES0):
                nc.scalar.activation(
                    out=sig0[:, g, :].rearrange("p (t j) -> p t j", j=PACK),
                    in_=y0_tiles[i][g][:].rearrange("p j t -> p t j"),
                    func=ACT.Abs,
                    scale=SCALE_Y0,
                )
            sig0_tiles[i] = sig0

        def sigmoid_y0(i, g):
            sig0 = sig0_tiles[i]
            nc.scalar.activation(out=sig0[:, g, :], in_=sig0[:, g, :], func=ACT.Sigmoid)

        def gate_y0(i):
            h0_tiles[i] = h0_pool.tile([P, PASSES0, BANK], BF16, name="h0", align_bytes=64)
            for g in range(PASSES0):
                nc.vector.scalar_tensor_tensor(
                    out=h0_tiles[i][:, g, :].rearrange("p (t j) -> p t j", j=PACK),
                    in0=y0_tiles[i][g][:].rearrange("p j t -> p t j"),
                    scalar=SCALE_Y0,
                    in1=sig0_tiles[i][:, g, :].rearrange("p (t j) -> p t j", j=PACK),
                    op0=ALU.mult,
                    op1=ALU.mult,
                )

        def second_scalar_matmul(i, on_scalar):
            words, scales = h_codes[i]
            o0_ps = ring.tile([P, U0], F32, name="o0_ps", tag="ring")
            for g in range(PASSES0):
                nc.tensor.matmul_mx(
                    out=o0_ps[:],
                    lhsT=words[:, g, :].bitcast(FP8X4),
                    lhsT_scale=scales[:, g, :],
                    rhs=w2_words[:, U0 * g : U0 * (g + 1)].bitcast(FP8X4),
                    rhs_scale=w2_scales[:, U0 * g : U0 * (g + 1)],
                    start=(g == 0),
                    stop=(g == PASSES0 - 1),
                )
            out_tiles[i] = o_pool.tile([P, X_COLS], F32, name="out_tile")
            o0 = out_tiles[i][:, 0:U0]
            if on_scalar:
                nc.scalar.mul(o0, o0_ps[:], SCALE_O0)
            else:
                nc.vector.tensor_scalar_mul(out=o0, in0=o0_ps[:], scalar1=SCALE_O0)

        def store(i):
            nc.sync.dma_start(out=out_groups[i // GROUP][:, i % GROUP, :], in_=out_tiles[i][:])

        def is_tile(i):
            return 0 <= i < TILES

        pools.enter_context(tc.manual_schedule())
        for step in range(-1, TILES + LAG + 2):
            front = step
            drain = front >= TILES + 0
            back = step - LAG
            o0_scalar = front > TILES + 3
            if (step + 1) % GROUP == 0 and (step + 1) // GROUP + 1 < TILES // GROUP:
                load_group((step + 1) // GROUP + 1)
            if is_tile(back):
                gate_y0(back)
            if is_tile(back + 1):
                sigmoid_abs_y0(back + 1)
                sigmoid_y0(back + 1, 0)
                if back + 1 in STARTS:
                    sigmoid_norm(back + 1)
            if is_tile(back - 1):
                second_scalar_matmul(back - 1, o0_scalar)
            if is_tile(back + 1):
                sigmoid_y0(back + 1, 1)
            if is_tile(back - 1):
                second_vector_matmul(back - 1)
                store(back - 1)
            if is_tile(front):
                square_last_component(front)
            if is_tile(front + 1):
                transpose_x(front + 1)
            if is_tile(front):
                keep_component(front, 0)
                keep_component(front, 1)
            if is_tile(back):
                gate_last_component(back)
                if drain:
                    gate_kept(back, 1, nc.vector)
            if is_tile(back + 2):
                first_scalar_matmul(back + 2)
            if is_tile(front - 1):
                square_kept(front - 1)
            if step == 0:
                for piece in range(4):
                    regroup_w1(piece)
            if step == min(9, LAG - 3):
                quantise_w1()
            if is_tile(back + 2) and back + 2 in STARTS:
                batch_roots(STARTS.index(back + 2))
            if is_tile(back + 2) and back + 2 not in STARTS:
                sigmoid_norm(back + 2)
            if is_tile(back):
                quantise_h(back)
            quantise_pair(back, front + 1)
            pairs[0] = None
            if step == LAG - 1:
                prepare_w2_w3()
            if is_tile(front - 2):
                for c in (1, 0):
                    add_square(front - 2, c)
            if is_tile(back + 1):
                gate_kept(back + 1, 0, nc.gpsimd, 1 if front + 1 >= TILES + 0 else 2)
